import numpy as np
import ml_dtypes

BF16 = ml_dtypes.bfloat16


def bf(x):
    return np.asarray(x, np.float32).astype(BF16)


def f32(x):
    return np.asarray(x, np.float32)


def f64(x):
    return np.asarray(x).astype(np.float64)


def striped(idx):
    return np.tile(idx.reshape(-1, 16).T, (8, 1))


C, S, NS, D, H, N = 128, 512, 64, 8, 8, 512
EPS = 1e-5
SELU_ALPHA = 1.6732632423543772
SELU_SCALE = 1.0507009873554805


def selu(t):
    return SELU_SCALE * (np.maximum(t, 0.0) + SELU_ALPHA * (np.exp(np.minimum(t, 0.0)) - 1.0))


def batchnorm(t, gamma, beta):
    m = t.mean(axis=0, keepdims=True)
    var = ((t - m) ** 2).mean(axis=0, keepdims=True)
    return (t - m) / np.sqrt(var + EPS) * gamma + beta


def setup_inputs():
    s1 = 1.0 / np.sqrt(D)
    s2 = 1.0 / np.sqrt(H)
    return {"x": f32(np.random.standard_normal((C, S))),
            "w1": f32(np.random.uniform(-s1, s1, (H, N))),
            "gamma1": f32(1.0 + 0.1 * np.random.standard_normal((1, NS * H))),
            "beta1": f32(0.1 * np.random.standard_normal((1, NS * H))),
            "w2": f32(np.random.uniform(-s2, s2, (H, NS * H))),
            "gamma2": f32(1.0 + 0.1 * np.random.standard_normal((1, NS * H))),
            "beta2": f32(0.1 * np.random.standard_normal((1, NS * H))),
            "w3": f32(np.random.uniform(-s2, s2, (1, NS * H))),
            "b3": f32(np.random.uniform(-s2, s2, (1, NS))),
            "offs": striped(np.random.permutation(np.tile(np.arange(S), 2))[:N])}


def reference(x, w1, gamma1, beta1, w2, gamma2, beta2, w3, b3, offs):
    idx = offs[:16].T.reshape(-1)
    xg = f64(x)[:, idx]
    a = (xg[:, None, :] * f64(w1)[None, :, :]).reshape(C, H, NS, D).sum(axis=3)
    a = a.transpose(0, 2, 1).reshape(C, NS * H)
    u = selu(batchnorm(a, f64(gamma1), f64(beta1)))
    e = (u[:, None, :] * f64(w2)[None, :, :]).reshape(C, H, NS, H).sum(axis=3)
    e = e.transpose(0, 2, 1).reshape(C, NS * H)
    y = selu(batchnorm(e, f64(gamma2), f64(beta2)))
    z = (y * f64(w3)).reshape(C, NS, H).sum(axis=2) + f64(b3)
    res = z.copy()
    res[:, -1] = 1.0 / (1.0 + np.exp(-z[:, -1]))
    return res

@@ -1,0 +1,202 @@
+import math
+
+import concourse.masks as masks
+import concourse.mybir as mybir
+
+F32 = mybir.dt.float32
+U16 = mybir.dt.uint16
+ALU = mybir.AluOpType
+FUNC = mybir.ActivationFunctionType
+AXIS = mybir.AxisListType
+
+RECORDS = 128
+GRAPH_NODES = 512
+NODES = 64
+PARENTS = 8
+HIDDEN = 8
+BLOCKS = 4
+BLOCK_NODES = NODES // BLOCKS
+BLOCK_UNITS = BLOCK_NODES * HIDDEN
+BLOCK_ENTRIES = BLOCK_NODES * PARENTS
+ENTRIES_PER_COLUMN = 16
+
+EPS = 1e-5
+SELU_ALPHA = 1.6732632423543772
+SELU_SCALE = 1.0507009873554805
+
+W2_ROWS = 0
+W3_ROW = 8
+GAMMA_ROWS = (9, 11)
+BETA_ROWS = (10, 12)
+PARAM_ROWS = 13
+PARAM_SLOT = 16
+
+FLOPS = 2 * RECORDS * NODES * (PARENTS * HIDDEN + HIDDEN * HIDDEN + HIDDEN)
+
+
+def batchnorm_selu(nc, small, halves, source, gamma_pair, beta_pair, eps, minus_half, ln_alpha):
+    stats = small.tile([BLOCK_UNITS, 6], F32, name="stats")
+    nc.vector.bn_stats(stats[:], source[:])
+    mean_var = small.tile([BLOCK_UNITS, 2], F32, name="mean_var")
+    nc.vector.bn_aggr(mean_var[:], stats[:])
+
+    var_eps = small.tile([BLOCK_UNITS, 1], F32, name="var_eps")
+    nc.gpsimd.tensor_scalar_add(var_eps[:], mean_var[:, 1:2], eps)
+    rstd = small.tile([BLOCK_UNITS, 1], F32, name="rstd")
+    nc.gpsimd.tensor_tensor(rstd[:], var_eps[:], minus_half[:], ALU.pow)
+
+    scales = small.tile([BLOCK_UNITS, 2], F32, name="scales")
+    nc.gpsimd.tensor_scalar_mul(scales[:], gamma_pair, rstd[:, 0:1])
+    shifts = small.tile([BLOCK_UNITS, 2], F32, name="shifts")
+    nc.vector.scalar_tensor_tensor(
+        out=shifts[:], in0=scales[:], scalar=mean_var[:, 0:1], in1=beta_pair, op0=ALU.mult, op1=ALU.add
+    )
+
+    rise = halves.tile([BLOCK_UNITS, RECORDS], F32, name="rise")
+    nc.scalar.activation(rise[:], source[:], FUNC.Relu, bias=shifts[:, 0:1], scale=scales[:, 1:2])
+    fall = halves.tile([BLOCK_UNITS, RECORDS], F32, name="fall")
+    nc.scalar.activation(fall[:], source[:], FUNC.Relu, bias=shifts[:, 1:2], scale=scales[:, 0:1])
+    decay = halves.tile([BLOCK_UNITS, RECORDS], F32, name="decay")
+    nc.scalar.activation(decay[:], fall[:], FUNC.Exp, bias=ln_alpha[:], scale=-1.0)
+    return rise, decay
+
+
+def tile_customnetwork_kernel(tc, x, w1, gamma1, beta1, w2, gamma2, beta2, w3, b3, offs, out):
+    nc = tc.nc
+    with (
+        tc.tile_pool(name="held", bufs=1) as held,
+        tc.tile_pool(name="per_block", bufs=BLOCKS) as per_block,
+        tc.tile_pool(name="halves", bufs=4) as halves,
+        tc.tile_pool(name="small", bufs=4) as small,
+        tc.psum_pool(name="once_ps", bufs=1) as once_ps,
+        tc.psum_pool(name="layer_ps", bufs=2) as layer_ps,
+    ):
+        offsets = held.tile([RECORDS, NODES * PARENTS // ENTRIES_PER_COLUMN], U16, name="offsets")
+        nc.sync.dma_start(offsets[:], offs)
+        table = held.tile([RECORDS, GRAPH_NODES], F32, name="table")
+        nc.sync.dma_start(table[:], x)
+
+        w1_copies = []
+        for b in range(BLOCKS):
+            w1_copy = held.tile([RECORDS, HIDDEN, BLOCK_ENTRIES], F32, name=f"w1_copy{b}")
+            queue = nc.scalar if b % 2 == 0 else nc.sync
+            block_of_w1 = w1[:, b * BLOCK_ENTRIES : (b + 1) * BLOCK_ENTRIES]
+            queue.dma_start(w1_copy[:], block_of_w1.unsqueeze(0).to_broadcast([RECORDS, HIDDEN, BLOCK_ENTRIES]))
+            w1_copies.append(w1_copy)
+            if b == 0:
+                params = held.tile([PARAM_ROWS, NODES * HIDDEN], F32, name="params")
+                nc.scalar.dma_start(params[W2_ROWS : W2_ROWS + HIDDEN, :], w2)
+                nc.scalar.dma_start(params[W3_ROW : W3_ROW + 1, :], w3)
+                for layer, (gamma, beta) in enumerate(((gamma1, beta1), (gamma2, beta2))):
+                    nc.scalar.dma_start(params[GAMMA_ROWS[layer] : GAMMA_ROWS[layer] + 1, :], gamma)
+                    nc.scalar.dma_start(params[BETA_ROWS[layer] : BETA_ROWS[layer] + 1, :], beta)
+                b3_copy = held.tile([RECORDS, NODES], F32, name="b3_copy")
+                nc.scalar.dma_start(b3_copy[:], b3.to_broadcast([RECORDS, NODES]))
+
+        identity = held.tile([128, 128], F32, name="identity")
+        masks.make_identity(nc, identity[:])
+        minus_half = held.tile([BLOCK_UNITS, 1], F32, name="minus_half")
+        nc.gpsimd.memset(minus_half[:], -0.5)
+        ln_alpha = held.tile([BLOCK_UNITS, 1], F32, name="ln_alpha")
+        nc.gpsimd.memset(ln_alpha[:], math.log(SELU_ALPHA))
+        selu_floor = held.tile([BLOCK_UNITS, RECORDS], F32, name="selu_floor")
+        nc.gpsimd.memset(selu_floor[:], -SELU_SCALE * SELU_ALPHA)
+        same_node = held.tile([BLOCK_UNITS, BLOCK_NODES], F32, name="same_node")
+        nc.vector.tensor_reduce(
+            out=same_node[:], in_=identity[:].rearrange("p (h i) -> p i h", i=BLOCK_NODES), axis=AXIS.X, op=ALU.add
+        )
+
+        params_by_unit = held.tile([PARAM_ROWS, NODES * HIDDEN], F32, name="params_by_unit")
+        nc.gpsimd.tensor_copy(
+            params_by_unit[:].rearrange("p (b h i) -> p b h i", b=BLOCKS, h=HIDDEN),
+            params[:].rearrange("p (b i h) -> p b h i", b=BLOCKS, h=HIDDEN),
+        )
+        signs = held.tile([PARAM_ROWS, 3, PARAM_SLOT], F32, name="signs")
+        nc.gpsimd.tensor_copy(
+            signs[:], identity[0:PARAM_ROWS, 0:PARAM_SLOT].unsqueeze(1).to_broadcast([PARAM_ROWS, 3, PARAM_SLOT])
+        )
+        nc.gpsimd.tensor_scalar_mul(signs[:, 1, :], signs[:, 1, :], -1.0)
+        columns_ps = once_ps.tile([BLOCK_UNITS, BLOCKS, 3 * PARAM_SLOT], F32, name="columns_ps")
+        for b in range(BLOCKS):
+            nc.tensor.matmul(
+                columns_ps[:, b, :],
+                lhsT=params_by_unit[:, b * BLOCK_UNITS : (b + 1) * BLOCK_UNITS],
+                rhs=signs[:].rearrange("p s c -> p (s c)"),
+                start=True,
+                stop=True,
+            )
+        columns = held.tile([BLOCK_UNITS, BLOCKS, 3, PARAM_SLOT], F32, name="columns")
+        nc.scalar.copy(columns[:].rearrange("p b s c -> p (b s c)"), columns_ps[:].rearrange("p b c -> p (b c)"))
+
+        w2_wide = held.tile([BLOCK_UNITS, BLOCKS, HIDDEN, BLOCK_NODES], F32, name="w2_wide")
+        w3_wide = held.tile([BLOCK_UNITS, BLOCKS, BLOCK_NODES], F32, name="w3_wide")
+        for b in range(BLOCKS):
+            nc.gpsimd.tensor_tensor(
+                w2_wide[:, b],
+                same_node[:].unsqueeze(1).to_broadcast([BLOCK_UNITS, HIDDEN, BLOCK_NODES]),
+                columns[:, b, 0, W2_ROWS : W2_ROWS + HIDDEN].unsqueeze(2).to_broadcast([BLOCK_UNITS, HIDDEN, BLOCK_NODES]),
+                ALU.mult,
+            )
+            nc.gpsimd.tensor_scalar_mul(w3_wide[:, b, :], same_node[:], columns[:, b, 0, W3_ROW : W3_ROW + 1])
+
+        floor_ps = once_ps.tile([RECORDS, NODES], F32, name="floor_ps")
+        for b in range(BLOCKS):
+            nc.tensor.matmul(
+                floor_ps[:, b * BLOCK_NODES : (b + 1) * BLOCK_NODES],
+                lhsT=selu_floor[:],
+                rhs=w3_wide[:, b, :],
+                start=True,
+                stop=True,
+            )
+        z_bias = held.tile([RECORDS, NODES], F32, name="z_bias")
+        nc.vector.tensor_tensor(z_bias[:], b3_copy[:], floor_ps[:], ALU.add)
+
+        z_ps = once_ps.tile([RECORDS, NODES], F32, name="z_ps")
+        for b in range(BLOCKS):
+            piece = offsets[:, b * BLOCK_ENTRIES // ENTRIES_PER_COLUMN : (b + 1) * BLOCK_ENTRIES // ENTRIES_PER_COLUMN]
+            products = per_block.tile([RECORDS, HIDDEN * BLOCK_ENTRIES], F32, name="products")
+            for h in range(HIDDEN):
+                nc.vector.tensor_tensor(
+                    products[:, h * BLOCK_ENTRIES : (h + 1) * BLOCK_ENTRIES],
+                    table[:].indirect(piece),
+                    w1_copies[b][:, h, :],
+                    ALU.mult,
+                )
+            by_parent = products[:].rearrange("r (u d) -> r u d", d=PARENTS)
+            a_ps = layer_ps.tile([BLOCK_UNITS, RECORDS], F32, name="a_ps")
+            for d in range(PARENTS):
+                nc.tensor.matmul(
+                    a_ps[:],
+                    lhsT=by_parent[:, :, d],
+                    rhs=identity[:],
+                    is_transpose=True,
+                    start=(d == 0),
+                    stop=(d == PARENTS - 1),
+                )
+            rise, decay = batchnorm_selu(
+                nc, small, halves, a_ps,
+                columns[:, b, 1:3, GAMMA_ROWS[0]], columns[:, b, 0:2, BETA_ROWS[0]], EPS, minus_half, ln_alpha,
+            )
+
+            w2_block = w2_wide[:, b].rearrange("p k j -> p (k j)")
+            e_ps = layer_ps.tile([BLOCK_UNITS, RECORDS], F32, name="e_ps")
+            nc.tensor.matmul(e_ps[:], lhsT=w2_block, rhs=rise[:], start=True, stop=False)
+            nc.tensor.matmul(e_ps[:], lhsT=w2_block, rhs=decay[:], start=False, stop=True)
+            rise, decay = batchnorm_selu(
+                nc, small, halves, e_ps,
+                columns[:, b, 1:3, GAMMA_ROWS[1]], columns[:, b, 0:2, BETA_ROWS[1]], EPS / SELU_SCALE**2,
+                minus_half, ln_alpha,
+            )
+
+            z_block = z_ps[:, b * BLOCK_NODES : (b + 1) * BLOCK_NODES]
+            nc.tensor.matmul(z_block, lhsT=rise[:], rhs=w3_wide[:, b, :], start=True, stop=False)
+            nc.tensor.matmul(z_block, lhsT=decay[:], rhs=w3_wide[:, b, :], start=False, stop=True)
+
+        result = held.tile([RECORDS, NODES], F32, name="result")
+        nc.vector.scalar_tensor_tensor(
+            out=result[:], in0=z_ps[:], scalar=SELU_SCALE, in1=z_bias[:], op0=ALU.mult, op1=ALU.add
+        )
+        tanh_half = held.tile([RECORDS, 1], F32, name="tanh_half")
+        nc.scalar.activation(tanh_half[:], result[:, NODES - 1 : NODES], FUNC.Tanh, scale=0.5)
+        nc.vector.tensor_scalar(result[:, NODES - 1 : NODES], tanh_half[:], 0.5, 0.5, op0=ALU.mult, op1=ALU.add)
+        nc.sync.dma_start(out, result[:])

@@ -39,23 +39,24 @@ def batchnorm_selu(nc, small, halves, source, gamma_pair, beta_pair, eps, minus_
     nc.vector.bn_stats(stats[:], source[:])
     mean_var = small.tile([BLOCK_UNITS, 2], F32, name="mean_var")
     nc.vector.bn_aggr(mean_var[:], stats[:])
-
     var_eps = small.tile([BLOCK_UNITS, 1], F32, name="var_eps")
-    nc.gpsimd.tensor_scalar_add(var_eps[:], mean_var[:, 1:2], eps)
+    nc.vector.tensor_scalar_add(var_eps[:], mean_var[:, 1:2], eps)
+
     rstd = small.tile([BLOCK_UNITS, 1], F32, name="rstd")
     nc.gpsimd.tensor_tensor(rstd[:], var_eps[:], minus_half[:], ALU.pow)
 
+    mean_gamma = small.tile([BLOCK_UNITS, 2], F32, name="mean_gamma")
+    nc.scalar.activation(mean_gamma[:], gamma_pair, FUNC.Copy, scale=mean_var[:, 0:1])
     scales = small.tile([BLOCK_UNITS, 2], F32, name="scales")
-    nc.gpsimd.tensor_scalar_mul(scales[:], gamma_pair, rstd[:, 0:1])
+    nc.scalar.activation(scales[:], gamma_pair, FUNC.Copy, scale=rstd[:, 0:1])
     shifts = small.tile([BLOCK_UNITS, 2], F32, name="shifts")
-    nc.vector.scalar_tensor_tensor(
-        out=shifts[:], in0=scales[:], scalar=mean_var[:, 0:1], in1=beta_pair, op0=ALU.mult, op1=ALU.add
-    )
+    nc.scalar.activation(shifts[:, 0:1], mean_gamma[:, 1:2], FUNC.Identity, bias=beta_pair[:, 0:1], scale=rstd[:, 0:1])
+    nc.scalar.activation(shifts[:, 1:2], mean_gamma[:, 0:1], FUNC.Identity, bias=beta_pair[:, 1:2], scale=rstd[:, 0:1])
 
     rise = halves.tile([BLOCK_UNITS, RECORDS], F32, name="rise")
-    nc.scalar.activation(rise[:], source[:], FUNC.Relu, bias=shifts[:, 0:1], scale=scales[:, 1:2])
+    nc.scalar.activation(rise[:], source[:], FUNC.Relu, bias=shifts[:, 0:1], scale=scales[:, 0:1])
     fall = halves.tile([BLOCK_UNITS, RECORDS], F32, name="fall")
-    nc.scalar.activation(fall[:], source[:], FUNC.Relu, bias=shifts[:, 1:2], scale=scales[:, 0:1])
+    nc.scalar.activation(fall[:], source[:], FUNC.Relu, bias=shifts[:, 1:2], scale=scales[:, 1:2])
     decay = halves.tile([BLOCK_UNITS, RECORDS], F32, name="decay")
     nc.scalar.activation(decay[:], fall[:], FUNC.Exp, bias=ln_alpha[:], scale=-1.0)
     return rise, decay
@@ -111,12 +112,12 @@ def tile_customnetwork_kernel(tc, x, w1, gamma1, beta1, w2, gamma2, beta2, w3, b
             params_by_unit[:].rearrange("p (b h i) -> p b h i", b=BLOCKS, h=HIDDEN),
             params[:].rearrange("p (b i h) -> p b h i", b=BLOCKS, h=HIDDEN),
         )
-        signs = held.tile([PARAM_ROWS, 3, PARAM_SLOT], F32, name="signs")
+        signs = held.tile([PARAM_ROWS, 2, PARAM_SLOT], F32, name="signs")
         nc.gpsimd.tensor_copy(
-            signs[:], identity[0:PARAM_ROWS, 0:PARAM_SLOT].unsqueeze(1).to_broadcast([PARAM_ROWS, 3, PARAM_SLOT])
+            signs[:], identity[0:PARAM_ROWS, 0:PARAM_SLOT].unsqueeze(1).to_broadcast([PARAM_ROWS, 2, PARAM_SLOT])
         )
         nc.gpsimd.tensor_scalar_mul(signs[:, 1, :], signs[:, 1, :], -1.0)
-        columns_ps = once_ps.tile([BLOCK_UNITS, BLOCKS, 3 * PARAM_SLOT], F32, name="columns_ps")
+        columns_ps = once_ps.tile([BLOCK_UNITS, BLOCKS, 2 * PARAM_SLOT], F32, name="columns_ps")
         for b in range(BLOCKS):
             nc.tensor.matmul(
                 columns_ps[:, b, :],
@@ -125,7 +126,7 @@ def tile_customnetwork_kernel(tc, x, w1, gamma1, beta1, w2, gamma2, beta2, w3, b
                 start=True,
                 stop=True,
             )
-        columns = held.tile([BLOCK_UNITS, BLOCKS, 3, PARAM_SLOT], F32, name="columns")
+        columns = held.tile([BLOCK_UNITS, BLOCKS, 2, PARAM_SLOT], F32, name="columns")
         nc.scalar.copy(columns[:].rearrange("p b s c -> p (b s c)"), columns_ps[:].rearrange("p b c -> p (b c)"))
 
         w2_wide = held.tile([BLOCK_UNITS, BLOCKS, HIDDEN, BLOCK_NODES], F32, name="w2_wide")
@@ -152,45 +153,55 @@ def tile_customnetwork_kernel(tc, x, w1, gamma1, beta1, w2, gamma2, beta2, w3, b
         nc.vector.tensor_tensor(z_bias[:], b3_copy[:], floor_ps[:], ALU.add)
 
         z_ps = once_ps.tile([RECORDS, NODES], F32, name="z_ps")
-        for b in range(BLOCKS):
-            piece = offsets[:, b * BLOCK_ENTRIES // ENTRIES_PER_COLUMN : (b + 1) * BLOCK_ENTRIES // ENTRIES_PER_COLUMN]
-            products = per_block.tile([RECORDS, HIDDEN * BLOCK_ENTRIES], F32, name="products")
-            for h in range(HIDDEN):
-                nc.vector.tensor_tensor(
-                    products[:, h * BLOCK_ENTRIES : (h + 1) * BLOCK_ENTRIES],
-                    table[:].indirect(piece),
-                    w1_copies[b][:, h, :],
-                    ALU.mult,
-                )
-            by_parent = products[:].rearrange("r (u d) -> r u d", d=PARENTS)
-            a_ps = layer_ps.tile([BLOCK_UNITS, RECORDS], F32, name="a_ps")
-            for d in range(PARENTS):
-                nc.tensor.matmul(
-                    a_ps[:],
-                    lhsT=by_parent[:, :, d],
-                    rhs=identity[:],
-                    is_transpose=True,
-                    start=(d == 0),
-                    stop=(d == PARENTS - 1),
-                )
-            rise, decay = batchnorm_selu(
-                nc, small, halves, a_ps,
-                columns[:, b, 1:3, GAMMA_ROWS[0]], columns[:, b, 0:2, BETA_ROWS[0]], EPS, minus_half, ln_alpha,
-            )
+        a_tiles = []
+        e_tiles = []
+        for step in range(BLOCKS + 2):
+            if step < BLOCKS:
+                b = step
+                piece = offsets[:, b * BLOCK_ENTRIES // ENTRIES_PER_COLUMN : (b + 1) * BLOCK_ENTRIES // ENTRIES_PER_COLUMN]
+                products = per_block.tile([RECORDS, HIDDEN * BLOCK_ENTRIES], F32, name="products")
+                for h in range(HIDDEN):
+                    nc.vector.tensor_tensor(
+                        products[:, h * BLOCK_ENTRIES : (h + 1) * BLOCK_ENTRIES],
+                        table[:].indirect(piece),
+                        w1_copies[b][:, h, :],
+                        ALU.mult,
+                    )
+                by_parent = products[:].rearrange("r (u d) -> r u d", d=PARENTS)
+                a_ps = layer_ps.tile([BLOCK_UNITS, RECORDS], F32, name="a_ps")
+                for d in range(PARENTS):
+                    nc.tensor.matmul(
+                        a_ps[:],
+                        lhsT=by_parent[:, :, d],
+                        rhs=identity[:],
+                        is_transpose=True,
+                        start=(d == 0),
+                        stop=(d == PARENTS - 1),
+                    )
+                a_tiles.append(a_ps)
 
-            w2_block = w2_wide[:, b].rearrange("p k j -> p (k j)")
-            e_ps = layer_ps.tile([BLOCK_UNITS, RECORDS], F32, name="e_ps")
-            nc.tensor.matmul(e_ps[:], lhsT=w2_block, rhs=rise[:], start=True, stop=False)
-            nc.tensor.matmul(e_ps[:], lhsT=w2_block, rhs=decay[:], start=False, stop=True)
-            rise, decay = batchnorm_selu(
-                nc, small, halves, e_ps,
-                columns[:, b, 1:3, GAMMA_ROWS[1]], columns[:, b, 0:2, BETA_ROWS[1]], EPS / SELU_SCALE**2,
-                minus_half, ln_alpha,
-            )
+            if 0 <= step - 1 < BLOCKS:
+                b = step - 1
+                rise, decay = batchnorm_selu(
+                    nc, small, halves, a_tiles[b],
+                    columns[:, b, :, GAMMA_ROWS[0]], columns[:, b, :, BETA_ROWS[0]], EPS, minus_half, ln_alpha,
+                )
+                w2_block = w2_wide[:, b].rearrange("p k j -> p (k j)")
+                e_ps = layer_ps.tile([BLOCK_UNITS, RECORDS], F32, name="e_ps")
+                nc.tensor.matmul(e_ps[:], lhsT=w2_block, rhs=rise[:], start=True, stop=False)
+                nc.tensor.matmul(e_ps[:], lhsT=w2_block, rhs=decay[:], start=False, stop=True)
+                e_tiles.append(e_ps)
 
-            z_block = z_ps[:, b * BLOCK_NODES : (b + 1) * BLOCK_NODES]
-            nc.tensor.matmul(z_block, lhsT=rise[:], rhs=w3_wide[:, b, :], start=True, stop=False)
-            nc.tensor.matmul(z_block, lhsT=decay[:], rhs=w3_wide[:, b, :], start=False, stop=True)
+            if 0 <= step - 2 < BLOCKS:
+                b = step - 2
+                rise, decay = batchnorm_selu(
+                    nc, small, halves, e_tiles[b],
+                    columns[:, b, :, GAMMA_ROWS[1]], columns[:, b, :, BETA_ROWS[1]], EPS / SELU_SCALE**2,
+                    minus_half, ln_alpha,
+                )
+                z_block = z_ps[:, b * BLOCK_NODES : (b + 1) * BLOCK_NODES]
+                nc.tensor.matmul(z_block, lhsT=rise[:], rhs=w3_wide[:, b, :], start=True, stop=False)
+                nc.tensor.matmul(z_block, lhsT=decay[:], rhs=w3_wide[:, b, :], start=False, stop=True)
 
         result = held.tile([RECORDS, NODES], F32, name="result")
         nc.vector.scalar_tensor_tensor(

@@ -7,7 +7,6 @@ F32 = mybir.dt.float32
 U16 = mybir.dt.uint16
 ALU = mybir.AluOpType
 FUNC = mybir.ActivationFunctionType
-AXIS = mybir.AxisListType
 
 RECORDS = 128
 GRAPH_NODES = 512
@@ -34,36 +33,45 @@ PARAM_SLOT = 16
 FLOPS = 2 * RECORDS * NODES * (PARENTS * HIDDEN + HIDDEN * HIDDEN + HIDDEN)
 
 
-def batchnorm_selu(nc, small, halves, source, gamma_pair, beta_pair, eps, minus_half, ln_alpha):
+def statistics(nc, small, source, eps, minus_half):
     stats = small.tile([BLOCK_UNITS, 6], F32, name="stats")
     nc.vector.bn_stats(stats[:], source[:])
     mean_var = small.tile([BLOCK_UNITS, 2], F32, name="mean_var")
     nc.vector.bn_aggr(mean_var[:], stats[:])
     var_eps = small.tile([BLOCK_UNITS, 1], F32, name="var_eps")
     nc.vector.tensor_scalar_add(var_eps[:], mean_var[:, 1:2], eps)
-
     rstd = small.tile([BLOCK_UNITS, 1], F32, name="rstd")
     nc.gpsimd.tensor_tensor(rstd[:], var_eps[:], minus_half[:], ALU.pow)
+    return mean_var[:, 0:1], rstd[:, 0:1]
 
-    mean_gamma = small.tile([BLOCK_UNITS, 2], F32, name="mean_gamma")
-    nc.scalar.activation(mean_gamma[:], gamma_pair, FUNC.Copy, scale=mean_var[:, 0:1])
+
+def selu_halves(nc, small, halves, source, mean, rstd, gamma_pair, beta_pair, ln_alpha):
     scales = small.tile([BLOCK_UNITS, 2], F32, name="scales")
-    nc.scalar.activation(scales[:], gamma_pair, FUNC.Copy, scale=rstd[:, 0:1])
+    nc.vector.tensor_scalar_mul(scales[:], gamma_pair, rstd)
     shifts = small.tile([BLOCK_UNITS, 2], F32, name="shifts")
-    nc.scalar.activation(shifts[:, 0:1], mean_gamma[:, 1:2], FUNC.Identity, bias=beta_pair[:, 0:1], scale=rstd[:, 0:1])
-    nc.scalar.activation(shifts[:, 1:2], mean_gamma[:, 0:1], FUNC.Identity, bias=beta_pair[:, 1:2], scale=rstd[:, 0:1])
+    nc.vector.scalar_tensor_tensor(out=shifts[:], in0=scales[:], scalar=mean, in1=beta_pair, op0=ALU.mult, op1=ALU.add)
 
     rise = halves.tile([BLOCK_UNITS, RECORDS], F32, name="rise")
-    nc.scalar.activation(rise[:], source[:], FUNC.Relu, bias=shifts[:, 0:1], scale=scales[:, 0:1])
+    nc.scalar.activation(rise[:], source[:], FUNC.Relu, bias=shifts[:, 0:1], scale=scales[:, 1:2])
     fall = halves.tile([BLOCK_UNITS, RECORDS], F32, name="fall")
-    nc.scalar.activation(fall[:], source[:], FUNC.Relu, bias=shifts[:, 1:2], scale=scales[:, 1:2])
+    nc.scalar.activation(fall[:], source[:], FUNC.Relu, bias=shifts[:, 1:2], scale=scales[:, 0:1])
     decay = halves.tile([BLOCK_UNITS, RECORDS], F32, name="decay")
     nc.scalar.activation(decay[:], fall[:], FUNC.Exp, bias=ln_alpha[:], scale=-1.0)
     return rise, decay
 
 
+def look_up(nc, products, table, offsets, w1_copy, b, units):
+    columns_per_block = BLOCK_ENTRIES // ENTRIES_PER_COLUMN
+    piece = offsets[:, b * columns_per_block : (b + 1) * columns_per_block]
+    for h in units:
+        nc.vector.tensor_tensor(
+            products[:, h * BLOCK_ENTRIES : (h + 1) * BLOCK_ENTRIES], table[:].indirect(piece), w1_copy[:, h, :], ALU.mult
+        )
+
+
 def tile_customnetwork_kernel(tc, x, w1, gamma1, beta1, w2, gamma2, beta2, w3, b3, offs, out):
     nc = tc.nc
+    half = HIDDEN // 2
     with (
         tc.tile_pool(name="held", bufs=1) as held,
         tc.tile_pool(name="per_block", bufs=BLOCKS) as per_block,
@@ -80,9 +88,9 @@ def tile_customnetwork_kernel(tc, x, w1, gamma1, beta1, w2, gamma2, beta2, w3, b
         w1_copies = []
         for b in range(BLOCKS):
             w1_copy = held.tile([RECORDS, HIDDEN, BLOCK_ENTRIES], F32, name=f"w1_copy{b}")
-            queue = nc.scalar if b % 2 == 0 else nc.sync
-            block_of_w1 = w1[:, b * BLOCK_ENTRIES : (b + 1) * BLOCK_ENTRIES]
-            queue.dma_start(w1_copy[:], block_of_w1.unsqueeze(0).to_broadcast([RECORDS, HIDDEN, BLOCK_ENTRIES]))
+            block_of_w1 = w1[:, b * BLOCK_ENTRIES : (b + 1) * BLOCK_ENTRIES].unsqueeze(0)
+            nc.scalar.dma_start(w1_copy[:, :half, :], block_of_w1[:, :half, :].to_broadcast([RECORDS, half, BLOCK_ENTRIES]))
+            nc.sync.dma_start(w1_copy[:, half:, :], block_of_w1[:, half:, :].to_broadcast([RECORDS, half, BLOCK_ENTRIES]))
             w1_copies.append(w1_copy)
             if b == 0:
                 params = held.tile([PARAM_ROWS, NODES * HIDDEN], F32, name="params")
@@ -91,8 +99,8 @@ def tile_customnetwork_kernel(tc, x, w1, gamma1, beta1, w2, gamma2, beta2, w3, b
                 for layer, (gamma, beta) in enumerate(((gamma1, beta1), (gamma2, beta2))):
                     nc.scalar.dma_start(params[GAMMA_ROWS[layer] : GAMMA_ROWS[layer] + 1, :], gamma)
                     nc.scalar.dma_start(params[BETA_ROWS[layer] : BETA_ROWS[layer] + 1, :], beta)
-                b3_copy = held.tile([RECORDS, NODES], F32, name="b3_copy")
-                nc.scalar.dma_start(b3_copy[:], b3.to_broadcast([RECORDS, NODES]))
+        b3_copy = held.tile([RECORDS, NODES], F32, name="b3_copy")
+        nc.scalar.dma_start(b3_copy[:], b3.to_broadcast([RECORDS, NODES]))
 
         identity = held.tile([128, 128], F32, name="identity")
         masks.make_identity(nc, identity[:])
@@ -100,24 +108,27 @@ def tile_customnetwork_kernel(tc, x, w1, gamma1, beta1, w2, gamma2, beta2, w3, b
         nc.gpsimd.memset(minus_half[:], -0.5)
         ln_alpha = held.tile([BLOCK_UNITS, 1], F32, name="ln_alpha")
         nc.gpsimd.memset(ln_alpha[:], math.log(SELU_ALPHA))
-        selu_floor = held.tile([BLOCK_UNITS, RECORDS], F32, name="selu_floor")
-        nc.gpsimd.memset(selu_floor[:], -SELU_SCALE * SELU_ALPHA)
-        same_node = held.tile([BLOCK_UNITS, BLOCK_NODES], F32, name="same_node")
-        nc.vector.tensor_reduce(
-            out=same_node[:], in_=identity[:].rearrange("p (h i) -> p i h", i=BLOCK_NODES), axis=AXIS.X, op=ALU.add
+        minus_alpha = held.tile([BLOCK_UNITS, RECORDS], F32, name="minus_alpha")
+        nc.gpsimd.memset(minus_alpha[:], -SELU_ALPHA)
+        signs = held.tile([PARAM_ROWS, 3, PARAM_SLOT], F32, name="signs")
+        nc.gpsimd.tensor_copy(
+            signs[:], identity[0:PARAM_ROWS, 0:PARAM_SLOT].unsqueeze(1).to_broadcast([PARAM_ROWS, 3, PARAM_SLOT])
         )
+        nc.gpsimd.tensor_scalar_mul(signs[:, 1, :], signs[:, 1, :], -1.0)
+        same_node = held.tile([BLOCK_UNITS, BLOCK_NODES], F32, name="same_node")
+        nc.gpsimd.memset(same_node[:], 0.0)
+        for h in range(HIDDEN):
+            nc.gpsimd.affine_select(
+                out=same_node[:], in_=same_node[:], compare_op=ALU.not_equal, fill=1.0,
+                base=-BLOCK_NODES * h, pattern=[[-1, BLOCK_NODES]], channel_multiplier=1,
+            )
 
         params_by_unit = held.tile([PARAM_ROWS, NODES * HIDDEN], F32, name="params_by_unit")
         nc.gpsimd.tensor_copy(
             params_by_unit[:].rearrange("p (b h i) -> p b h i", b=BLOCKS, h=HIDDEN),
             params[:].rearrange("p (b i h) -> p b h i", b=BLOCKS, h=HIDDEN),
         )
-        signs = held.tile([PARAM_ROWS, 2, PARAM_SLOT], F32, name="signs")
-        nc.gpsimd.tensor_copy(
-            signs[:], identity[0:PARAM_ROWS, 0:PARAM_SLOT].unsqueeze(1).to_broadcast([PARAM_ROWS, 2, PARAM_SLOT])
-        )
-        nc.gpsimd.tensor_scalar_mul(signs[:, 1, :], signs[:, 1, :], -1.0)
-        columns_ps = once_ps.tile([BLOCK_UNITS, BLOCKS, 2 * PARAM_SLOT], F32, name="columns_ps")
+        columns_ps = once_ps.tile([BLOCK_UNITS, BLOCKS, 3 * PARAM_SLOT], F32, name="columns_ps")
         for b in range(BLOCKS):
             nc.tensor.matmul(
                 columns_ps[:, b, :],
@@ -126,47 +137,46 @@ def tile_customnetwork_kernel(tc, x, w1, gamma1, beta1, w2, gamma2, beta2, w3, b
                 start=True,
                 stop=True,
             )
-        columns = held.tile([BLOCK_UNITS, BLOCKS, 2, PARAM_SLOT], F32, name="columns")
+        columns = held.tile([BLOCK_UNITS, BLOCKS, 3, PARAM_SLOT], F32, name="columns")
         nc.scalar.copy(columns[:].rearrange("p b s c -> p (b s c)"), columns_ps[:].rearrange("p b c -> p (b c)"))
-
         w2_wide = held.tile([BLOCK_UNITS, BLOCKS, HIDDEN, BLOCK_NODES], F32, name="w2_wide")
         w3_wide = held.tile([BLOCK_UNITS, BLOCKS, BLOCK_NODES], F32, name="w3_wide")
-        for b in range(BLOCKS):
-            nc.gpsimd.tensor_tensor(
-                w2_wide[:, b],
-                same_node[:].unsqueeze(1).to_broadcast([BLOCK_UNITS, HIDDEN, BLOCK_NODES]),
-                columns[:, b, 0, W2_ROWS : W2_ROWS + HIDDEN].unsqueeze(2).to_broadcast([BLOCK_UNITS, HIDDEN, BLOCK_NODES]),
-                ALU.mult,
-            )
-            nc.gpsimd.tensor_scalar_mul(w3_wide[:, b, :], same_node[:], columns[:, b, 0, W3_ROW : W3_ROW + 1])
-
-        floor_ps = once_ps.tile([RECORDS, NODES], F32, name="floor_ps")
-        for b in range(BLOCKS):
-            nc.tensor.matmul(
-                floor_ps[:, b * BLOCK_NODES : (b + 1) * BLOCK_NODES],
-                lhsT=selu_floor[:],
-                rhs=w3_wide[:, b, :],
-                start=True,
-                stop=True,
-            )
-        z_bias = held.tile([RECORDS, NODES], F32, name="z_bias")
-        nc.vector.tensor_tensor(z_bias[:], b3_copy[:], floor_ps[:], ALU.add)
 
         z_ps = once_ps.tile([RECORDS, NODES], F32, name="z_ps")
-        a_tiles = []
-        e_tiles = []
-        for step in range(BLOCKS + 2):
+        products_tiles, a_tiles, a_stats, e_tiles, e_stats = [], [], [], [], []
+        for step in range(BLOCKS + 3):
             if step < BLOCKS:
                 b = step
-                piece = offsets[:, b * BLOCK_ENTRIES // ENTRIES_PER_COLUMN : (b + 1) * BLOCK_ENTRIES // ENTRIES_PER_COLUMN]
+                nc.gpsimd.tensor_tensor(
+                    w2_wide[:, b],
+                    same_node[:].unsqueeze(1).to_broadcast([BLOCK_UNITS, HIDDEN, BLOCK_NODES]),
+                    columns[:, b, 0, W2_ROWS : W2_ROWS + HIDDEN].unsqueeze(2).to_broadcast([BLOCK_UNITS, HIDDEN, BLOCK_NODES]),
+                    ALU.mult,
+                )
+                nc.gpsimd.tensor_scalar_mul(w3_wide[:, b, :], same_node[:], columns[:, b, 0, W3_ROW : W3_ROW + 1])
                 products = per_block.tile([RECORDS, HIDDEN * BLOCK_ENTRIES], F32, name="products")
-                for h in range(HIDDEN):
-                    nc.vector.tensor_tensor(
-                        products[:, h * BLOCK_ENTRIES : (h + 1) * BLOCK_ENTRIES],
-                        table[:].indirect(piece),
-                        w1_copies[b][:, h, :],
-                        ALU.mult,
-                    )
+                products_tiles.append(products)
+                look_up(nc, products, table, offsets, w1_copies[b], b, range(0, half))
+
+            if 0 <= step - 3 < BLOCKS:
+                b = step - 3
+                mean, rstd = e_stats[b]
+                rise, decay = selu_halves(
+                    nc, small, halves, e_tiles[b], mean, rstd,
+                    columns[:, b, 1:3, GAMMA_ROWS[1]], columns[:, b, 0:2, BETA_ROWS[1]], ln_alpha,
+                )
+                z_block = z_ps[:, b * BLOCK_NODES : (b + 1) * BLOCK_NODES]
+                nc.tensor.matmul(z_block, lhsT=minus_alpha[:], rhs=w3_wide[:, b, :], start=True, stop=False)
+                nc.tensor.matmul(z_block, lhsT=rise[:], rhs=w3_wide[:, b, :], start=False, stop=False)
+                nc.tensor.matmul(z_block, lhsT=decay[:], rhs=w3_wide[:, b, :], start=False, stop=True)
+
+            if 0 <= step - 1 < BLOCKS:
+                a_stats.append(statistics(nc, small, a_tiles[step - 1], EPS, minus_half))
+
+            if step < BLOCKS:
+                b = step
+                products = products_tiles[b]
+                look_up(nc, products, table, offsets, w1_copies[b], b, range(half, HIDDEN))
                 by_parent = products[:].rearrange("r (u d) -> r u d", d=PARENTS)
                 a_ps = layer_ps.tile([BLOCK_UNITS, RECORDS], F32, name="a_ps")
                 for d in range(PARENTS):
@@ -182,9 +192,10 @@ def tile_customnetwork_kernel(tc, x, w1, gamma1, beta1, w2, gamma2, beta2, w3, b
 
             if 0 <= step - 1 < BLOCKS:
                 b = step - 1
-                rise, decay = batchnorm_selu(
-                    nc, small, halves, a_tiles[b],
-                    columns[:, b, :, GAMMA_ROWS[0]], columns[:, b, :, BETA_ROWS[0]], EPS, minus_half, ln_alpha,
+                mean, rstd = a_stats[b]
+                rise, decay = selu_halves(
+                    nc, small, halves, a_tiles[b], mean, rstd,
+                    columns[:, b, 1:3, GAMMA_ROWS[0]], columns[:, b, 0:2, BETA_ROWS[0]], ln_alpha,
                 )
                 w2_block = w2_wide[:, b].rearrange("p k j -> p (k j)")
                 e_ps = layer_ps.tile([BLOCK_UNITS, RECORDS], F32, name="e_ps")
@@ -193,19 +204,11 @@ def tile_customnetwork_kernel(tc, x, w1, gamma1, beta1, w2, gamma2, beta2, w3, b
                 e_tiles.append(e_ps)
 
             if 0 <= step - 2 < BLOCKS:
-                b = step - 2
-                rise, decay = batchnorm_selu(
-                    nc, small, halves, e_tiles[b],
-                    columns[:, b, :, GAMMA_ROWS[1]], columns[:, b, :, BETA_ROWS[1]], EPS / SELU_SCALE**2,
-                    minus_half, ln_alpha,
-                )
-                z_block = z_ps[:, b * BLOCK_NODES : (b + 1) * BLOCK_NODES]
-                nc.tensor.matmul(z_block, lhsT=rise[:], rhs=w3_wide[:, b, :], start=True, stop=False)
-                nc.tensor.matmul(z_block, lhsT=decay[:], rhs=w3_wide[:, b, :], start=False, stop=True)
+                e_stats.append(statistics(nc, small, e_tiles[step - 2], EPS / SELU_SCALE**2, minus_half))
 
         result = held.tile([RECORDS, NODES], F32, name="result")
         nc.vector.scalar_tensor_tensor(
-            out=result[:], in0=z_ps[:], scalar=SELU_SCALE, in1=z_bias[:], op0=ALU.mult, op1=ALU.add
+            out=result[:], in0=z_ps[:], scalar=SELU_SCALE, in1=b3_copy[:], op0=ALU.mult, op1=ALU.add
         )
         tanh_half = held.tile([RECORDS, 1], F32, name="tanh_half")
         nc.scalar.activation(tanh_half[:], result[:, NODES - 1 : NODES], FUNC.Tanh, scale=0.5)

@@ -23,50 +23,48 @@ EPS = 1e-5
 SELU_ALPHA = 1.6732632423543772
 SELU_SCALE = 1.0507009873554805
 
-W2_ROWS = 0
-W3_ROW = 8
-GAMMA_ROWS = (9, 11)
-BETA_ROWS = (10, 12)
-PARAM_ROWS = 13
-PARAM_SLOT = 16
+NODE_ROWS = 0
+W2_ROWS = 16
+W3_ROW = 24
+GAMMA_ROWS = (25, 27)
+BETA_ROWS = (26, 28)
+PARAM_ROWS = 29
+PARAM_SLOT = 32
 
 FLOPS = 2 * RECORDS * NODES * (PARENTS * HIDDEN + HIDDEN * HIDDEN + HIDDEN)
 
 
-def statistics(nc, small, source, eps, minus_half):
-    stats = small.tile([BLOCK_UNITS, 6], F32, name="stats")
-    nc.vector.bn_stats(stats[:], source[:])
-    mean_var = small.tile([BLOCK_UNITS, 2], F32, name="mean_var")
-    nc.vector.bn_aggr(mean_var[:], stats[:])
-    var_eps = small.tile([BLOCK_UNITS, 1], F32, name="var_eps")
-    nc.vector.tensor_scalar_add(var_eps[:], mean_var[:, 1:2], eps)
-    rstd = small.tile([BLOCK_UNITS, 1], F32, name="rstd")
+def selu_of_batchnorm(nc, small, work, sources, gamma, beta_pair, eps, minus_half):
+    mean_var = small.tile([BLOCK_UNITS, BLOCKS, 2], F32, name="mean_var")
+    for b in range(BLOCKS):
+        stats = small.tile([BLOCK_UNITS, 6], F32, name="stats")
+        nc.vector.bn_stats(stats[:], sources[b][:])
+        nc.vector.bn_aggr(mean_var[:, b, :], stats[:])
+    mean = mean_var[:, :, 0]
+
+    var_eps = small.tile([BLOCK_UNITS, BLOCKS], F32, name="var_eps")
+    nc.vector.tensor_scalar_add(var_eps[:], mean_var[:, :, 1], eps)
+    rstd = small.tile([BLOCK_UNITS, BLOCKS], F32, name="rstd")
     nc.gpsimd.tensor_tensor(rstd[:], var_eps[:], minus_half[:], ALU.pow)
-    return mean_var[:, 0:1], rstd[:, 0:1]
+    scale = small.tile([BLOCK_UNITS, BLOCKS], F32, name="scale")
+    nc.vector.tensor_tensor(scale[:], rstd[:], gamma, ALU.mult)
+    mean_scale = small.tile([BLOCK_UNITS, BLOCKS], F32, name="mean_scale")
+    nc.vector.tensor_tensor(mean_scale[:], mean, scale[:], ALU.mult)
+    shift_pair = small.tile([BLOCK_UNITS, BLOCKS, 2], F32, name="shift_pair")
+    nc.vector.tensor_tensor(
+        shift_pair[:], beta_pair, mean_scale[:].unsqueeze(2).to_broadcast([BLOCK_UNITS, BLOCKS, 2]), ALU.subtract
+    )
 
-
-def selu_halves(nc, small, halves, source, mean, rstd, gamma_pair, beta_pair, ln_alpha):
-    scales = small.tile([BLOCK_UNITS, 2], F32, name="scales")
-    nc.vector.tensor_scalar_mul(scales[:], gamma_pair, rstd)
-    shifts = small.tile([BLOCK_UNITS, 2], F32, name="shifts")
-    nc.vector.scalar_tensor_tensor(out=shifts[:], in0=scales[:], scalar=mean, in1=beta_pair, op0=ALU.mult, op1=ALU.add)
-
-    rise = halves.tile([BLOCK_UNITS, RECORDS], F32, name="rise")
-    nc.scalar.activation(rise[:], source[:], FUNC.Relu, bias=shifts[:, 0:1], scale=scales[:, 1:2])
-    fall = halves.tile([BLOCK_UNITS, RECORDS], F32, name="fall")
-    nc.scalar.activation(fall[:], source[:], FUNC.Relu, bias=shifts[:, 1:2], scale=scales[:, 0:1])
-    decay = halves.tile([BLOCK_UNITS, RECORDS], F32, name="decay")
-    nc.scalar.activation(decay[:], fall[:], FUNC.Exp, bias=ln_alpha[:], scale=-1.0)
-    return rise, decay
-
-
-def look_up(nc, products, table, offsets, w1_copy, b, units):
-    columns_per_block = BLOCK_ENTRIES // ENTRIES_PER_COLUMN
-    piece = offsets[:, b * columns_per_block : (b + 1) * columns_per_block]
-    for h in units:
-        nc.vector.tensor_tensor(
-            products[:, h * BLOCK_ENTRIES : (h + 1) * BLOCK_ENTRIES], table[:].indirect(piece), w1_copy[:, h, :], ALU.mult
-        )
+    results = []
+    for b in range(BLOCKS):
+        rise = work.tile([BLOCK_UNITS, RECORDS], F32, name="rise")
+        nc.scalar.activation(rise[:], sources[b][:], FUNC.Relu, bias=shift_pair[:, b, 0:1], scale=scale[:, b : b + 1])
+        grown = work.tile([BLOCK_UNITS, RECORDS], F32, name="grown")
+        nc.scalar.activation(grown[:], sources[b][:], FUNC.Exp, bias=shift_pair[:, b, 1:2], scale=scale[:, b : b + 1])
+        both = work.tile([BLOCK_UNITS, RECORDS], F32, name="both")
+        nc.vector.scalar_tensor_tensor(out=both[:], in0=grown[:], scalar=SELU_ALPHA, in1=rise[:], op0=ALU.min, op1=ALU.add)
+        results.append(both)
+    return results
 
 
 def tile_customnetwork_kernel(tc, x, w1, gamma1, beta1, w2, gamma2, beta2, w3, b3, offs, out):
@@ -74,137 +72,129 @@ def tile_customnetwork_kernel(tc, x, w1, gamma1, beta1, w2, gamma2, beta2, w3, b
     half = HIDDEN // 2
     with (
         tc.tile_pool(name="held", bufs=1) as held,
-        tc.tile_pool(name="per_block", bufs=BLOCKS) as per_block,
-        tc.tile_pool(name="halves", bufs=4) as halves,
-        tc.tile_pool(name="small", bufs=4) as small,
+        tc.tile_pool(name="work", bufs=BLOCKS) as work,
+        tc.tile_pool(name="small", bufs=BLOCKS) as small,
         tc.psum_pool(name="once_ps", bufs=1) as once_ps,
-        tc.psum_pool(name="layer_ps", bufs=2) as layer_ps,
+        tc.psum_pool(name="layer_ps", bufs=6) as layer_ps,
     ):
         offsets = held.tile([RECORDS, NODES * PARENTS // ENTRIES_PER_COLUMN], U16, name="offsets")
         nc.sync.dma_start(offsets[:], offs)
         table = held.tile([RECORDS, GRAPH_NODES], F32, name="table")
         nc.sync.dma_start(table[:], x)
 
-        w1_copies = []
+        w1_copies = [held.tile([RECORDS, HIDDEN, BLOCK_ENTRIES], F32, name=f"w1_copy{b}") for b in range(BLOCKS)]
+        params = held.tile([PARAM_ROWS, NODES * HIDDEN], F32, name="params")
+        b3_copy = held.tile([RECORDS, NODES], F32, name="b3_copy")
         for b in range(BLOCKS):
-            w1_copy = held.tile([RECORDS, HIDDEN, BLOCK_ENTRIES], F32, name=f"w1_copy{b}")
-            block_of_w1 = w1[:, b * BLOCK_ENTRIES : (b + 1) * BLOCK_ENTRIES].unsqueeze(0)
-            nc.scalar.dma_start(w1_copy[:, :half, :], block_of_w1[:, :half, :].to_broadcast([RECORDS, half, BLOCK_ENTRIES]))
-            nc.sync.dma_start(w1_copy[:, half:, :], block_of_w1[:, half:, :].to_broadcast([RECORDS, half, BLOCK_ENTRIES]))
-            w1_copies.append(w1_copy)
-            if b == 0:
-                params = held.tile([PARAM_ROWS, NODES * HIDDEN], F32, name="params")
+            if b == BLOCKS // 2:
                 nc.scalar.dma_start(params[W2_ROWS : W2_ROWS + HIDDEN, :], w2)
-                nc.scalar.dma_start(params[W3_ROW : W3_ROW + 1, :], w3)
+                nc.sync.dma_start(params[W3_ROW : W3_ROW + 1, :], w3)
                 for layer, (gamma, beta) in enumerate(((gamma1, beta1), (gamma2, beta2))):
                     nc.scalar.dma_start(params[GAMMA_ROWS[layer] : GAMMA_ROWS[layer] + 1, :], gamma)
-                    nc.scalar.dma_start(params[BETA_ROWS[layer] : BETA_ROWS[layer] + 1, :], beta)
-        b3_copy = held.tile([RECORDS, NODES], F32, name="b3_copy")
+                    nc.sync.dma_start(params[BETA_ROWS[layer] : BETA_ROWS[layer] + 1, :], beta)
+            block_of_w1 = w1[:, b * BLOCK_ENTRIES : (b + 1) * BLOCK_ENTRIES].unsqueeze(0)
+            nc.scalar.dma_start(
+                w1_copies[b][:, :half, :], block_of_w1[:, :half, :].to_broadcast([RECORDS, half, BLOCK_ENTRIES])
+            )
+            nc.sync.dma_start(
+                w1_copies[b][:, half:, :], block_of_w1[:, half:, :].to_broadcast([RECORDS, half, BLOCK_ENTRIES])
+            )
         nc.scalar.dma_start(b3_copy[:], b3.to_broadcast([RECORDS, NODES]))
 
         identity = held.tile([128, 128], F32, name="identity")
         masks.make_identity(nc, identity[:])
-        minus_half = held.tile([BLOCK_UNITS, 1], F32, name="minus_half")
-        nc.gpsimd.memset(minus_half[:], -0.5)
-        ln_alpha = held.tile([BLOCK_UNITS, 1], F32, name="ln_alpha")
-        nc.gpsimd.memset(ln_alpha[:], math.log(SELU_ALPHA))
+        minus_half = held.tile([BLOCK_UNITS, BLOCKS], F32, name="minus_half")
+        nc.vector.memset(minus_half[:], -0.5)
         minus_alpha = held.tile([BLOCK_UNITS, RECORDS], F32, name="minus_alpha")
-        nc.gpsimd.memset(minus_alpha[:], -SELU_ALPHA)
-        signs = held.tile([PARAM_ROWS, 3, PARAM_SLOT], F32, name="signs")
-        nc.gpsimd.tensor_copy(
-            signs[:], identity[0:PARAM_ROWS, 0:PARAM_SLOT].unsqueeze(1).to_broadcast([PARAM_ROWS, 3, PARAM_SLOT])
-        )
-        nc.gpsimd.tensor_scalar_mul(signs[:, 1, :], signs[:, 1, :], -1.0)
-        same_node = held.tile([BLOCK_UNITS, BLOCK_NODES], F32, name="same_node")
-        nc.gpsimd.memset(same_node[:], 0.0)
-        for h in range(HIDDEN):
-            nc.gpsimd.affine_select(
-                out=same_node[:], in_=same_node[:], compare_op=ALU.not_equal, fill=1.0,
-                base=-BLOCK_NODES * h, pattern=[[-1, BLOCK_NODES]], channel_multiplier=1,
-            )
+        nc.vector.memset(minus_alpha[:], -SELU_ALPHA)
 
+        nc.scalar.copy(
+            params[NODE_ROWS : NODE_ROWS + BLOCK_NODES, :].rearrange("p (b i h) -> p b i h", b=BLOCKS, h=HIDDEN),
+            identity[0:BLOCK_NODES, 0:BLOCK_NODES]
+            .unsqueeze(1)
+            .unsqueeze(3)
+            .to_broadcast([BLOCK_NODES, BLOCKS, BLOCK_NODES, HIDDEN]),
+        )
         params_by_unit = held.tile([PARAM_ROWS, NODES * HIDDEN], F32, name="params_by_unit")
-        nc.gpsimd.tensor_copy(
+        nc.scalar.copy(
             params_by_unit[:].rearrange("p (b h i) -> p b h i", b=BLOCKS, h=HIDDEN),
             params[:].rearrange("p (b i h) -> p b h i", b=BLOCKS, h=HIDDEN),
         )
-        columns_ps = once_ps.tile([BLOCK_UNITS, BLOCKS, 3 * PARAM_SLOT], F32, name="columns_ps")
+        columns_ps = once_ps.tile([BLOCK_UNITS, BLOCKS, PARAM_SLOT], F32, name="columns_ps")
         for b in range(BLOCKS):
             nc.tensor.matmul(
                 columns_ps[:, b, :],
                 lhsT=params_by_unit[:, b * BLOCK_UNITS : (b + 1) * BLOCK_UNITS],
-                rhs=signs[:].rearrange("p s c -> p (s c)"),
+                rhs=identity[0:PARAM_ROWS, 0:PARAM_SLOT],
                 start=True,
                 stop=True,
             )
-        columns = held.tile([BLOCK_UNITS, BLOCKS, 3, PARAM_SLOT], F32, name="columns")
-        nc.scalar.copy(columns[:].rearrange("p b s c -> p (b s c)"), columns_ps[:].rearrange("p b c -> p (b c)"))
-        w2_wide = held.tile([BLOCK_UNITS, BLOCKS, HIDDEN, BLOCK_NODES], F32, name="w2_wide")
-        w3_wide = held.tile([BLOCK_UNITS, BLOCKS, BLOCK_NODES], F32, name="w3_wide")
+        columns = held.tile([BLOCK_UNITS, BLOCKS, PARAM_SLOT], F32, name="columns")
+        nc.scalar.copy(columns[:], columns_ps[:])
+        beta_pairs = []
+        for layer in range(2):
+            beta_pair = held.tile([BLOCK_UNITS, BLOCKS, 2], F32, name=f"beta_pair{layer}")
+            nc.scalar.copy(beta_pair[:, :, 0], columns[:, :, BETA_ROWS[layer]])
+            nc.scalar.add(beta_pair[:, :, 1], columns[:, :, BETA_ROWS[layer]], math.log(SELU_ALPHA))
+            beta_pairs.append(beta_pair)
+        same_node = columns[:, 0, NODE_ROWS : NODE_ROWS + BLOCK_NODES]
 
-        z_ps = once_ps.tile([RECORDS, NODES], F32, name="z_ps")
-        products_tiles, a_tiles, a_stats, e_tiles, e_stats = [], [], [], [], []
-        for step in range(BLOCKS + 3):
-            if step < BLOCKS:
-                b = step
-                nc.gpsimd.tensor_tensor(
-                    w2_wide[:, b],
-                    same_node[:].unsqueeze(1).to_broadcast([BLOCK_UNITS, HIDDEN, BLOCK_NODES]),
-                    columns[:, b, 0, W2_ROWS : W2_ROWS + HIDDEN].unsqueeze(2).to_broadcast([BLOCK_UNITS, HIDDEN, BLOCK_NODES]),
+        columns_per_block = BLOCK_ENTRIES // ENTRIES_PER_COLUMN
+        a_tiles = []
+        for b in range(BLOCKS):
+            piece = offsets[:, b * columns_per_block : (b + 1) * columns_per_block]
+            products = work.tile([RECORDS, HIDDEN * BLOCK_ENTRIES], F32, name="products")
+            for h in range(HIDDEN):
+                nc.vector.tensor_tensor(
+                    products[:, h * BLOCK_ENTRIES : (h + 1) * BLOCK_ENTRIES],
+                    table[:].indirect(piece),
+                    w1_copies[b][:, h, :],
                     ALU.mult,
                 )
-                nc.gpsimd.tensor_scalar_mul(w3_wide[:, b, :], same_node[:], columns[:, b, 0, W3_ROW : W3_ROW + 1])
-                products = per_block.tile([RECORDS, HIDDEN * BLOCK_ENTRIES], F32, name="products")
-                products_tiles.append(products)
-                look_up(nc, products, table, offsets, w1_copies[b], b, range(0, half))
-
-            if 0 <= step - 3 < BLOCKS:
-                b = step - 3
-                mean, rstd = e_stats[b]
-                rise, decay = selu_halves(
-                    nc, small, halves, e_tiles[b], mean, rstd,
-                    columns[:, b, 1:3, GAMMA_ROWS[1]], columns[:, b, 0:2, BETA_ROWS[1]], ln_alpha,
+            by_parent = products[:].rearrange("r (u d) -> r u d", d=PARENTS)
+            a_ps = layer_ps.tile([BLOCK_UNITS, RECORDS], F32, name="sums")
+            for d in range(PARENTS):
+                nc.tensor.matmul(
+                    a_ps[:],
+                    lhsT=by_parent[:, :, d],
+                    rhs=identity[:],
+                    is_transpose=True,
+                    start=(d == 0),
+                    stop=(d == PARENTS - 1),
                 )
-                z_block = z_ps[:, b * BLOCK_NODES : (b + 1) * BLOCK_NODES]
-                nc.tensor.matmul(z_block, lhsT=minus_alpha[:], rhs=w3_wide[:, b, :], start=True, stop=False)
-                nc.tensor.matmul(z_block, lhsT=rise[:], rhs=w3_wide[:, b, :], start=False, stop=False)
-                nc.tensor.matmul(z_block, lhsT=decay[:], rhs=w3_wide[:, b, :], start=False, stop=True)
+            a_tiles.append(a_ps)
 
-            if 0 <= step - 1 < BLOCKS:
-                a_stats.append(statistics(nc, small, a_tiles[step - 1], EPS, minus_half))
+        w2_wide = held.tile([BLOCK_UNITS, BLOCKS, HIDDEN, BLOCK_NODES], F32, name="w2_wide")
+        w3_wide = held.tile([BLOCK_UNITS, BLOCKS, BLOCK_NODES], F32, name="w3_wide")
+        for b in range(BLOCKS):
+            nc.vector.tensor_tensor(
+                w2_wide[:, b],
+                same_node.unsqueeze(1).to_broadcast([BLOCK_UNITS, HIDDEN, BLOCK_NODES]),
+                columns[:, b, W2_ROWS : W2_ROWS + HIDDEN].unsqueeze(2).to_broadcast([BLOCK_UNITS, HIDDEN, BLOCK_NODES]),
+                ALU.mult,
+            )
+            nc.vector.tensor_scalar_mul(w3_wide[:, b, :], same_node, columns[:, b, W3_ROW : W3_ROW + 1])
 
-            if step < BLOCKS:
-                b = step
-                products = products_tiles[b]
-                look_up(nc, products, table, offsets, w1_copies[b], b, range(half, HIDDEN))
-                by_parent = products[:].rearrange("r (u d) -> r u d", d=PARENTS)
-                a_ps = layer_ps.tile([BLOCK_UNITS, RECORDS], F32, name="a_ps")
-                for d in range(PARENTS):
-                    nc.tensor.matmul(
-                        a_ps[:],
-                        lhsT=by_parent[:, :, d],
-                        rhs=identity[:],
-                        is_transpose=True,
-                        start=(d == 0),
-                        stop=(d == PARENTS - 1),
-                    )
-                a_tiles.append(a_ps)
+        u_tiles = selu_of_batchnorm(
+            nc, small, work, a_tiles, columns[:, :, GAMMA_ROWS[0]], beta_pairs[0][:], EPS, minus_half
+        )
 
-            if 0 <= step - 1 < BLOCKS:
-                b = step - 1
-                mean, rstd = a_stats[b]
-                rise, decay = selu_halves(
-                    nc, small, halves, a_tiles[b], mean, rstd,
-                    columns[:, b, 1:3, GAMMA_ROWS[0]], columns[:, b, 0:2, BETA_ROWS[0]], ln_alpha,
-                )
-                w2_block = w2_wide[:, b].rearrange("p k j -> p (k j)")
-                e_ps = layer_ps.tile([BLOCK_UNITS, RECORDS], F32, name="e_ps")
-                nc.tensor.matmul(e_ps[:], lhsT=w2_block, rhs=rise[:], start=True, stop=False)
-                nc.tensor.matmul(e_ps[:], lhsT=w2_block, rhs=decay[:], start=False, stop=True)
-                e_tiles.append(e_ps)
+        e_tiles = []
+        for b in range(BLOCKS):
+            e_ps = layer_ps.tile([BLOCK_UNITS, RECORDS], F32, name="sums")
+            nc.tensor.matmul(
+                e_ps[:], lhsT=w2_wide[:, b].rearrange("p k j -> p (k j)"), rhs=u_tiles[b][:], start=True, stop=True
+            )
+            e_tiles.append(e_ps)
+        y_tiles = selu_of_batchnorm(
+            nc, small, work, e_tiles, columns[:, :, GAMMA_ROWS[1]], beta_pairs[1][:], EPS / SELU_SCALE**2, minus_half
+        )
 
-            if 0 <= step - 2 < BLOCKS:
-                e_stats.append(statistics(nc, small, e_tiles[step - 2], EPS / SELU_SCALE**2, minus_half))
+        z_ps = once_ps.tile([RECORDS, NODES], F32, name="z_ps")
+        for b in range(BLOCKS):
+            z_block = z_ps[:, b * BLOCK_NODES : (b + 1) * BLOCK_NODES]
+            nc.tensor.matmul(z_block, lhsT=minus_alpha[:], rhs=w3_wide[:, b, :], start=True, stop=False)
+            nc.tensor.matmul(z_block, lhsT=y_tiles[b][:], rhs=w3_wide[:, b, :], start=False, stop=True)
 
         result = held.tile([RECORDS, NODES], F32, name="result")
         nc.vector.scalar_tensor_tensor(

@@ -17,6 +17,7 @@ BLOCKS = 4
 BLOCK_NODES = NODES // BLOCKS
 BLOCK_UNITS = BLOCK_NODES * HIDDEN
 BLOCK_ENTRIES = BLOCK_NODES * PARENTS
+GROUP = 2
 ENTRIES_PER_COLUMN = 16
 
 EPS = 1e-5
@@ -26,34 +27,44 @@ SELU_SCALE = 1.0507009873554805
 NODE_ROWS = 0
 W2_ROWS = 16
 W3_ROW = 24
-GAMMA_ROWS = (25, 27)
-BETA_ROWS = (26, 28)
+GAMMA_ROWS = (25, 26)
+BETA_ROWS = (27, 28)
 PARAM_ROWS = 29
 PARAM_SLOT = 32
 
 FLOPS = 2 * RECORDS * NODES * (PARENTS * HIDDEN + HIDDEN * HIDDEN + HIDDEN)
 
 
-def selu_of_batchnorm(nc, small, work, sources, gamma, beta_pair, eps, minus_half):
+def selu_of_batchnorm(nc, small, work, sources, gamma, minus_gamma, beta_pair, eps, minus_half):
     mean_var = small.tile([BLOCK_UNITS, BLOCKS, 2], F32, name="mean_var")
-    for b in range(BLOCKS):
-        stats = small.tile([BLOCK_UNITS, 6], F32, name="stats")
-        nc.vector.bn_stats(stats[:], sources[b][:])
-        nc.vector.bn_aggr(mean_var[:, b, :], stats[:])
-    mean = mean_var[:, :, 0]
-
-    var_eps = small.tile([BLOCK_UNITS, BLOCKS], F32, name="var_eps")
-    nc.vector.tensor_scalar_add(var_eps[:], mean_var[:, :, 1], eps)
     rstd = small.tile([BLOCK_UNITS, BLOCKS], F32, name="rstd")
-    nc.gpsimd.tensor_tensor(rstd[:], var_eps[:], minus_half[:], ALU.pow)
+    minus_mean_gamma = small.tile([BLOCK_UNITS, BLOCKS], F32, name="minus_mean_gamma")
+    for first in range(0, BLOCKS, GROUP):
+        group = slice(first, first + GROUP)
+        stats = small.tile([BLOCK_UNITS, GROUP, 6], F32, name="stats")
+        for g in range(GROUP):
+            nc.vector.bn_stats(stats[:, g, :], sources[first + g][:])
+        for g in range(GROUP):
+            nc.vector.bn_aggr(mean_var[:, first + g, :], stats[:, g, :])
+        var_eps = small.tile([BLOCK_UNITS, GROUP], F32, name="var_eps")
+        nc.vector.tensor_scalar_add(var_eps[:], mean_var[:, group, 1], eps)
+        nc.gpsimd.tensor_tensor(rstd[:, group], var_eps[:], minus_half[:], ALU.pow)
+        nc.vector.tensor_tensor(minus_mean_gamma[:, group], mean_var[:, group, 0], minus_gamma[:, group], ALU.mult)
+
     scale = small.tile([BLOCK_UNITS, BLOCKS], F32, name="scale")
-    nc.vector.tensor_tensor(scale[:], rstd[:], gamma, ALU.mult)
-    mean_scale = small.tile([BLOCK_UNITS, BLOCKS], F32, name="mean_scale")
-    nc.vector.tensor_tensor(mean_scale[:], mean, scale[:], ALU.mult)
     shift_pair = small.tile([BLOCK_UNITS, BLOCKS, 2], F32, name="shift_pair")
-    nc.vector.tensor_tensor(
-        shift_pair[:], beta_pair, mean_scale[:].unsqueeze(2).to_broadcast([BLOCK_UNITS, BLOCKS, 2]), ALU.subtract
-    )
+    for first in range(0, BLOCKS, GROUP):
+        group = slice(first, first + GROUP)
+        nc.vector.tensor_tensor(scale[:, group], rstd[:, group], gamma[:, group], ALU.mult)
+        for b in range(first, first + GROUP):
+            nc.vector.scalar_tensor_tensor(
+                out=shift_pair[:, b, :],
+                in0=minus_mean_gamma[:, b : b + 1].to_broadcast([BLOCK_UNITS, 2]),
+                scalar=rstd[:, b : b + 1],
+                in1=beta_pair[:, b, :],
+                op0=ALU.mult,
+                op1=ALU.add,
+            )
 
     results = []
     for b in range(BLOCKS):
@@ -83,27 +94,27 @@ def tile_customnetwork_kernel(tc, x, w1, gamma1, beta1, w2, gamma2, beta2, w3, b
         nc.sync.dma_start(table[:], x)
 
         w1_copies = [held.tile([RECORDS, HIDDEN, BLOCK_ENTRIES], F32, name=f"w1_copy{b}") for b in range(BLOCKS)]
+        w1_blocks = [w1[:, b * BLOCK_ENTRIES : (b + 1) * BLOCK_ENTRIES].unsqueeze(0) for b in range(BLOCKS)]
+        nc.scalar.dma_start(
+            w1_copies[0][:, :half, :], w1_blocks[0][:, :half, :].to_broadcast([RECORDS, half, BLOCK_ENTRIES])
+        )
+        nc.sync.dma_start(
+            w1_copies[0][:, half:, :], w1_blocks[0][:, half:, :].to_broadcast([RECORDS, half, BLOCK_ENTRIES])
+        )
+        for b in range(1, BLOCKS):
+            nc.sync.dma_start(w1_copies[b][:], w1_blocks[b].to_broadcast([RECORDS, HIDDEN, BLOCK_ENTRIES]))
         params = held.tile([PARAM_ROWS, NODES * HIDDEN], F32, name="params")
+        nc.scalar.dma_start(params[W2_ROWS : W2_ROWS + HIDDEN, :], w2)
+        nc.scalar.dma_start(params[W3_ROW : W3_ROW + 1, :], w3)
+        for layer, (gamma, beta) in enumerate(((gamma1, beta1), (gamma2, beta2))):
+            nc.scalar.dma_start(params[GAMMA_ROWS[layer] : GAMMA_ROWS[layer] + 1, :], gamma)
+            nc.scalar.dma_start(params[BETA_ROWS[layer] : BETA_ROWS[layer] + 1, :], beta)
         b3_copy = held.tile([RECORDS, NODES], F32, name="b3_copy")
-        for b in range(BLOCKS):
-            if b == BLOCKS // 2:
-                nc.scalar.dma_start(params[W2_ROWS : W2_ROWS + HIDDEN, :], w2)
-                nc.sync.dma_start(params[W3_ROW : W3_ROW + 1, :], w3)
-                for layer, (gamma, beta) in enumerate(((gamma1, beta1), (gamma2, beta2))):
-                    nc.scalar.dma_start(params[GAMMA_ROWS[layer] : GAMMA_ROWS[layer] + 1, :], gamma)
-                    nc.sync.dma_start(params[BETA_ROWS[layer] : BETA_ROWS[layer] + 1, :], beta)
-            block_of_w1 = w1[:, b * BLOCK_ENTRIES : (b + 1) * BLOCK_ENTRIES].unsqueeze(0)
-            nc.scalar.dma_start(
-                w1_copies[b][:, :half, :], block_of_w1[:, :half, :].to_broadcast([RECORDS, half, BLOCK_ENTRIES])
-            )
-            nc.sync.dma_start(
-                w1_copies[b][:, half:, :], block_of_w1[:, half:, :].to_broadcast([RECORDS, half, BLOCK_ENTRIES])
-            )
-        nc.scalar.dma_start(b3_copy[:], b3.to_broadcast([RECORDS, NODES]))
+        nc.sync.dma_start(b3_copy[:], b3.to_broadcast([RECORDS, NODES]))
 
         identity = held.tile([128, 128], F32, name="identity")
         masks.make_identity(nc, identity[:])
-        minus_half = held.tile([BLOCK_UNITS, BLOCKS], F32, name="minus_half")
+        minus_half = held.tile([BLOCK_UNITS, GROUP], F32, name="minus_half")
         nc.vector.memset(minus_half[:], -0.5)
         minus_alpha = held.tile([BLOCK_UNITS, RECORDS], F32, name="minus_alpha")
         nc.vector.memset(minus_alpha[:], -SELU_ALPHA)
@@ -131,12 +142,12 @@ def tile_customnetwork_kernel(tc, x, w1, gamma1, beta1, w2, gamma2, beta2, w3, b
             )
         columns = held.tile([BLOCK_UNITS, BLOCKS, PARAM_SLOT], F32, name="columns")
         nc.scalar.copy(columns[:], columns_ps[:])
-        beta_pairs = []
-        for layer in range(2):
-            beta_pair = held.tile([BLOCK_UNITS, BLOCKS, 2], F32, name=f"beta_pair{layer}")
-            nc.scalar.copy(beta_pair[:, :, 0], columns[:, :, BETA_ROWS[layer]])
-            nc.scalar.add(beta_pair[:, :, 1], columns[:, :, BETA_ROWS[layer]], math.log(SELU_ALPHA))
-            beta_pairs.append(beta_pair)
+        both_betas = columns[:, :, BETA_ROWS[0] : BETA_ROWS[1] + 1]
+        beta_pairs = held.tile([BLOCK_UNITS, BLOCKS, 2, 2], F32, name="beta_pairs")
+        nc.scalar.copy(beta_pairs[:, :, :, 0], both_betas)
+        nc.scalar.add(beta_pairs[:, :, :, 1], both_betas, math.log(SELU_ALPHA))
+        minus_gammas = held.tile([BLOCK_UNITS, BLOCKS, 2], F32, name="minus_gammas")
+        nc.scalar.mul(minus_gammas[:], columns[:, :, GAMMA_ROWS[0] : GAMMA_ROWS[1] + 1], -1.0)
         same_node = columns[:, 0, NODE_ROWS : NODE_ROWS + BLOCK_NODES]
 
         columns_per_block = BLOCK_ENTRIES // ENTRIES_PER_COLUMN
@@ -166,17 +177,22 @@ def tile_customnetwork_kernel(tc, x, w1, gamma1, beta1, w2, gamma2, beta2, w3, b
 
         w2_wide = held.tile([BLOCK_UNITS, BLOCKS, HIDDEN, BLOCK_NODES], F32, name="w2_wide")
         w3_wide = held.tile([BLOCK_UNITS, BLOCKS, BLOCK_NODES], F32, name="w3_wide")
-        for b in range(BLOCKS):
-            nc.vector.tensor_tensor(
-                w2_wide[:, b],
-                same_node.unsqueeze(1).to_broadcast([BLOCK_UNITS, HIDDEN, BLOCK_NODES]),
-                columns[:, b, W2_ROWS : W2_ROWS + HIDDEN].unsqueeze(2).to_broadcast([BLOCK_UNITS, HIDDEN, BLOCK_NODES]),
-                ALU.mult,
-            )
-            nc.vector.tensor_scalar_mul(w3_wide[:, b, :], same_node, columns[:, b, W3_ROW : W3_ROW + 1])
+        nc.vector.tensor_tensor(
+            w2_wide[:],
+            same_node.unsqueeze(1).unsqueeze(1).to_broadcast([BLOCK_UNITS, BLOCKS, HIDDEN, BLOCK_NODES]),
+            columns[:, :, W2_ROWS : W2_ROWS + HIDDEN].unsqueeze(3).to_broadcast([BLOCK_UNITS, BLOCKS, HIDDEN, BLOCK_NODES]),
+            ALU.mult,
+        )
+        nc.vector.tensor_tensor(
+            w3_wide[:],
+            same_node.unsqueeze(1).to_broadcast([BLOCK_UNITS, BLOCKS, BLOCK_NODES]),
+            columns[:, :, W3_ROW : W3_ROW + 1].to_broadcast([BLOCK_UNITS, BLOCKS, BLOCK_NODES]),
+            ALU.mult,
+        )
 
         u_tiles = selu_of_batchnorm(
-            nc, small, work, a_tiles, columns[:, :, GAMMA_ROWS[0]], beta_pairs[0][:], EPS, minus_half
+            nc, small, work, a_tiles,
+            columns[:, :, GAMMA_ROWS[0]], minus_gammas[:, :, 0], beta_pairs[:, :, 0, :], EPS, minus_half,
         )
 
         e_tiles = []
@@ -187,7 +203,8 @@ def tile_customnetwork_kernel(tc, x, w1, gamma1, beta1, w2, gamma2, beta2, w3, b
             )
             e_tiles.append(e_ps)
         y_tiles = selu_of_batchnorm(
-            nc, small, work, e_tiles, columns[:, :, GAMMA_ROWS[1]], beta_pairs[1][:], EPS / SELU_SCALE**2, minus_half
+            nc, small, work, e_tiles,
+            columns[:, :, GAMMA_ROWS[1]], minus_gammas[:, :, 1], beta_pairs[:, :, 1, :], EPS / SELU_SCALE**2, minus_half,
         )
 
         z_ps = once_ps.tile([RECORDS, NODES], F32, name="z_ps")

@@ -35,7 +35,7 @@ PARAM_SLOT = 32
 FLOPS = 2 * RECORDS * NODES * (PARENTS * HIDDEN + HIDDEN * HIDDEN + HIDDEN)
 
 
-def selu_of_batchnorm(nc, small, work, sources, gamma, minus_gamma, beta_pair, eps, minus_half):
+def normalisation(nc, small, sources, gamma, minus_gamma, beta_pair, eps, minus_half):
     mean_var = small.tile([BLOCK_UNITS, BLOCKS, 2], F32, name="mean_var")
     rstd = small.tile([BLOCK_UNITS, BLOCKS], F32, name="rstd")
     minus_mean_gamma = small.tile([BLOCK_UNITS, BLOCKS], F32, name="minus_mean_gamma")
@@ -65,7 +65,10 @@ def selu_of_batchnorm(nc, small, work, sources, gamma, minus_gamma, beta_pair, e
                 op0=ALU.mult,
                 op1=ALU.add,
             )
+    return scale, shift_pair
 
+
+def activation(nc, work, sources, scale, shift_pair):
     results = []
     for b in range(BLOCKS):
         rise = work.tile([BLOCK_UNITS, RECORDS], F32, name="rise")
@@ -88,16 +91,15 @@ def tile_customnetwork_kernel(tc, x, w1, gamma1, beta1, w2, gamma2, beta2, w3, b
         tc.psum_pool(name="once_ps", bufs=1) as once_ps,
         tc.psum_pool(name="layer_ps", bufs=6) as layer_ps,
     ):
-        offsets = held.tile([RECORDS, NODES * PARENTS // ENTRIES_PER_COLUMN], U16, name="offsets")
-        nc.sync.dma_start(offsets[:], offs)
-        table = held.tile([RECORDS, GRAPH_NODES], F32, name="table")
-        nc.sync.dma_start(table[:], x)
-
         w1_copies = [held.tile([RECORDS, HIDDEN, BLOCK_ENTRIES], F32, name=f"w1_copy{b}") for b in range(BLOCKS)]
         w1_blocks = [w1[:, b * BLOCK_ENTRIES : (b + 1) * BLOCK_ENTRIES].unsqueeze(0) for b in range(BLOCKS)]
-        nc.scalar.dma_start(
+        table = held.tile([RECORDS, GRAPH_NODES], F32, name="table")
+        offsets = held.tile([RECORDS, NODES * PARENTS // ENTRIES_PER_COLUMN], U16, name="offsets")
+        nc.scalar.dma_start(table[:], x)
+        nc.sync.dma_start(
             w1_copies[0][:, :half, :], w1_blocks[0][:, :half, :].to_broadcast([RECORDS, half, BLOCK_ENTRIES])
         )
+        nc.sync.dma_start(offsets[:], offs)
         nc.sync.dma_start(
             w1_copies[0][:, half:, :], w1_blocks[0][:, half:, :].to_broadcast([RECORDS, half, BLOCK_ENTRIES])
         )
@@ -148,6 +150,8 @@ def tile_customnetwork_kernel(tc, x, w1, gamma1, beta1, w2, gamma2, beta2, w3, b
         nc.scalar.add(beta_pairs[:, :, :, 1], both_betas, math.log(SELU_ALPHA))
         minus_gammas = held.tile([BLOCK_UNITS, BLOCKS, 2], F32, name="minus_gammas")
         nc.scalar.mul(minus_gammas[:], columns[:, :, GAMMA_ROWS[0] : GAMMA_ROWS[1] + 1], -1.0)
+        half_b3_last = held.tile([RECORDS, 1], F32, name="half_b3_last")
+        nc.scalar.mul(half_b3_last[:], b3_copy[:, NODES - 1 : NODES], 0.5)
         same_node = columns[:, 0, NODE_ROWS : NODE_ROWS + BLOCK_NODES]
 
         columns_per_block = BLOCK_ENTRIES // ENTRIES_PER_COLUMN
@@ -175,6 +179,10 @@ def tile_customnetwork_kernel(tc, x, w1, gamma1, beta1, w2, gamma2, beta2, w3, b
                 )
             a_tiles.append(a_ps)
 
+        scale, shift_pair = normalisation(
+            nc, small, a_tiles, columns[:, :, GAMMA_ROWS[0]], minus_gammas[:, :, 0], beta_pairs[:, :, 0, :], EPS, minus_half
+        )
+
         w2_wide = held.tile([BLOCK_UNITS, BLOCKS, HIDDEN, BLOCK_NODES], F32, name="w2_wide")
         w3_wide = held.tile([BLOCK_UNITS, BLOCKS, BLOCK_NODES], F32, name="w3_wide")
         nc.vector.tensor_tensor(
@@ -190,10 +198,7 @@ def tile_customnetwork_kernel(tc, x, w1, gamma1, beta1, w2, gamma2, beta2, w3, b
             ALU.mult,
         )
 
-        u_tiles = selu_of_batchnorm(
-            nc, small, work, a_tiles,
-            columns[:, :, GAMMA_ROWS[0]], minus_gammas[:, :, 0], beta_pairs[:, :, 0, :], EPS, minus_half,
-        )
+        u_tiles = activation(nc, work, a_tiles, scale, shift_pair)
 
         e_tiles = []
         for b in range(BLOCKS):
@@ -202,10 +207,11 @@ def tile_customnetwork_kernel(tc, x, w1, gamma1, beta1, w2, gamma2, beta2, w3, b
                 e_ps[:], lhsT=w2_wide[:, b].rearrange("p k j -> p (k j)"), rhs=u_tiles[b][:], start=True, stop=True
             )
             e_tiles.append(e_ps)
-        y_tiles = selu_of_batchnorm(
-            nc, small, work, e_tiles,
+        scale, shift_pair = normalisation(
+            nc, small, e_tiles,
             columns[:, :, GAMMA_ROWS[1]], minus_gammas[:, :, 1], beta_pairs[:, :, 1, :], EPS / SELU_SCALE**2, minus_half,
         )
+        y_tiles = activation(nc, work, e_tiles, scale, shift_pair)
 
         z_ps = once_ps.tile([RECORDS, NODES], F32, name="z_ps")
         for b in range(BLOCKS):
@@ -218,6 +224,8 @@ def tile_customnetwork_kernel(tc, x, w1, gamma1, beta1, w2, gamma2, beta2, w3, b
             out=result[:], in0=z_ps[:], scalar=SELU_SCALE, in1=b3_copy[:], op0=ALU.mult, op1=ALU.add
         )
         tanh_half = held.tile([RECORDS, 1], F32, name="tanh_half")
-        nc.scalar.activation(tanh_half[:], result[:, NODES - 1 : NODES], FUNC.Tanh, scale=0.5)
+        nc.scalar.activation(
+            tanh_half[:], z_ps[:, NODES - 1 : NODES], FUNC.Tanh, bias=half_b3_last[:], scale=0.5 * SELU_SCALE
+        )
         nc.vector.tensor_scalar(result[:, NODES - 1 : NODES], tanh_half[:], 0.5, 0.5, op0=ALU.mult, op1=ALU.add)
         nc.sync.dma_start(out, result[:])

@@ -17,7 +17,8 @@ BLOCKS = 4
 BLOCK_NODES = NODES // BLOCKS
 BLOCK_UNITS = BLOCK_NODES * HIDDEN
 BLOCK_ENTRIES = BLOCK_NODES * PARENTS
-GROUP = 2
+LAYERS = 2
+STATISTICS_AHEAD = 2
 ENTRIES_PER_COLUMN = 16
 
 EPS = 1e-5
@@ -35,50 +36,39 @@ PARAM_SLOT = 32
 FLOPS = 2 * RECORDS * NODES * (PARENTS * HIDDEN + HIDDEN * HIDDEN + HIDDEN)
 
 
-def normalisation(nc, small, sources, gamma, minus_gamma, beta_pair, eps, minus_half):
-    mean_var = small.tile([BLOCK_UNITS, BLOCKS, 2], F32, name="mean_var")
-    rstd = small.tile([BLOCK_UNITS, BLOCKS], F32, name="rstd")
-    minus_mean_gamma = small.tile([BLOCK_UNITS, BLOCKS], F32, name="minus_mean_gamma")
-    for first in range(0, BLOCKS, GROUP):
-        group = slice(first, first + GROUP)
-        stats = small.tile([BLOCK_UNITS, GROUP, 6], F32, name="stats")
-        for g in range(GROUP):
-            nc.vector.bn_stats(stats[:, g, :], sources[first + g][:])
-        for g in range(GROUP):
-            nc.vector.bn_aggr(mean_var[:, first + g, :], stats[:, g, :])
-        var_eps = small.tile([BLOCK_UNITS, GROUP], F32, name="var_eps")
-        nc.vector.tensor_scalar_add(var_eps[:], mean_var[:, group, 1], eps)
-        nc.gpsimd.tensor_tensor(rstd[:, group], var_eps[:], minus_half[:], ALU.pow)
-        nc.vector.tensor_tensor(minus_mean_gamma[:, group], mean_var[:, group, 0], minus_gamma[:, group], ALU.mult)
-
-    scale = small.tile([BLOCK_UNITS, BLOCKS], F32, name="scale")
-    shift_pair = small.tile([BLOCK_UNITS, BLOCKS, 2], F32, name="shift_pair")
-    for first in range(0, BLOCKS, GROUP):
-        group = slice(first, first + GROUP)
-        nc.vector.tensor_tensor(scale[:, group], rstd[:, group], gamma[:, group], ALU.mult)
-        for b in range(first, first + GROUP):
-            nc.vector.scalar_tensor_tensor(
-                out=shift_pair[:, b, :],
-                in0=minus_mean_gamma[:, b : b + 1].to_broadcast([BLOCK_UNITS, 2]),
-                scalar=rstd[:, b : b + 1],
-                in1=beta_pair[:, b, :],
-                op0=ALU.mult,
-                op1=ALU.add,
-            )
-    return scale, shift_pair
+def statistics(nc, small, source, minus_gamma, eps, minus_half):
+    stats = small.tile([BLOCK_UNITS, 6], F32, name="stats")
+    nc.vector.bn_stats(stats[:], source[:])
+    mean_var = small.tile([BLOCK_UNITS, 2], F32, name="mean_var")
+    nc.vector.bn_aggr(mean_var[:], stats[:])
+    var_eps = small.tile([BLOCK_UNITS, 1], F32, name="var_eps")
+    nc.vector.tensor_scalar_add(var_eps[:], mean_var[:, 1:2], eps)
+    rstd = small.tile([BLOCK_UNITS, 1], F32, name="rstd")
+    nc.gpsimd.tensor_tensor(rstd[:], var_eps[:], minus_half[:], ALU.pow)
+    minus_mean_gamma = small.tile([BLOCK_UNITS, 1], F32, name="minus_mean_gamma")
+    nc.scalar.activation(minus_mean_gamma[:], mean_var[:, 0:1], FUNC.Identity, scale=minus_gamma)
+    return rstd, minus_mean_gamma
 
 
-def activation(nc, work, sources, scale, shift_pair):
-    results = []
-    for b in range(BLOCKS):
-        rise = work.tile([BLOCK_UNITS, RECORDS], F32, name="rise")
-        nc.scalar.activation(rise[:], sources[b][:], FUNC.Relu, bias=shift_pair[:, b, 0:1], scale=scale[:, b : b + 1])
-        grown = work.tile([BLOCK_UNITS, RECORDS], F32, name="grown")
-        nc.scalar.activation(grown[:], sources[b][:], FUNC.Exp, bias=shift_pair[:, b, 1:2], scale=scale[:, b : b + 1])
-        both = work.tile([BLOCK_UNITS, RECORDS], F32, name="both")
-        nc.vector.scalar_tensor_tensor(out=both[:], in0=grown[:], scalar=SELU_ALPHA, in1=rise[:], op0=ALU.min, op1=ALU.add)
-        results.append(both)
-    return results
+def selu_parts(nc, small, work, source, rstd, minus_mean_gamma, gamma, beta_pair):
+    scale = small.tile([BLOCK_UNITS, 1], F32, name="scale")
+    nc.scalar.activation(scale[:], rstd[:], FUNC.Identity, scale=gamma)
+    shift_pair = small.tile([BLOCK_UNITS, 2], F32, name="shift_pair")
+    for j in range(2):
+        nc.scalar.activation(
+            shift_pair[:, j : j + 1], rstd[:], FUNC.Identity, bias=beta_pair[:, j : j + 1], scale=minus_mean_gamma[:]
+        )
+    rise = work.tile([BLOCK_UNITS, RECORDS], F32, name="rise")
+    nc.scalar.activation(rise[:], source[:], FUNC.Relu, bias=shift_pair[:, 0:1], scale=scale[:])
+    grown = work.tile([BLOCK_UNITS, RECORDS], F32, name="grown")
+    nc.scalar.activation(grown[:], source[:], FUNC.Exp, bias=shift_pair[:, 1:2], scale=scale[:])
+    return rise, grown
+
+
+def selu_sum(nc, work, rise, grown):
+    both = work.tile([BLOCK_UNITS, RECORDS], F32, name="both")
+    nc.vector.scalar_tensor_tensor(out=both[:], in0=grown[:], scalar=SELU_ALPHA, in1=rise[:], op0=ALU.min, op1=ALU.add)
+    return both
 
 
 def tile_customnetwork_kernel(tc, x, w1, gamma1, beta1, w2, gamma2, beta2, w3, b3, offs, out):
@@ -86,8 +76,8 @@ def tile_customnetwork_kernel(tc, x, w1, gamma1, beta1, w2, gamma2, beta2, w3, b
     half = HIDDEN // 2
     with (
         tc.tile_pool(name="held", bufs=1) as held,
-        tc.tile_pool(name="work", bufs=BLOCKS) as work,
-        tc.tile_pool(name="small", bufs=BLOCKS) as small,
+        tc.tile_pool(name="work", bufs=2 * BLOCKS) as work,
+        tc.tile_pool(name="small", bufs=2 * BLOCKS) as small,
         tc.psum_pool(name="once_ps", bufs=1) as once_ps,
         tc.psum_pool(name="layer_ps", bufs=6) as layer_ps,
     ):
@@ -116,7 +106,7 @@ def tile_customnetwork_kernel(tc, x, w1, gamma1, beta1, w2, gamma2, beta2, w3, b
 
         identity = held.tile([128, 128], F32, name="identity")
         masks.make_identity(nc, identity[:])
-        minus_half = held.tile([BLOCK_UNITS, GROUP], F32, name="minus_half")
+        minus_half = held.tile([BLOCK_UNITS, 1], F32, name="minus_half")
         nc.vector.memset(minus_half[:], -0.5)
         minus_alpha = held.tile([BLOCK_UNITS, RECORDS], F32, name="minus_alpha")
         nc.vector.memset(minus_alpha[:], -SELU_ALPHA)
@@ -179,10 +169,6 @@ def tile_customnetwork_kernel(tc, x, w1, gamma1, beta1, w2, gamma2, beta2, w3, b
                 )
             a_tiles.append(a_ps)
 
-        scale, shift_pair = normalisation(
-            nc, small, a_tiles, columns[:, :, GAMMA_ROWS[0]], minus_gammas[:, :, 0], beta_pairs[:, :, 0, :], EPS, minus_half
-        )
-
         w2_wide = held.tile([BLOCK_UNITS, BLOCKS, HIDDEN, BLOCK_NODES], F32, name="w2_wide")
         w3_wide = held.tile([BLOCK_UNITS, BLOCKS, BLOCK_NODES], F32, name="w3_wide")
         nc.vector.tensor_tensor(
@@ -198,26 +184,38 @@ def tile_customnetwork_kernel(tc, x, w1, gamma1, beta1, w2, gamma2, beta2, w3, b
             ALU.mult,
         )
 
-        u_tiles = activation(nc, work, a_tiles, scale, shift_pair)
-
-        e_tiles = []
-        for b in range(BLOCKS):
-            e_ps = layer_ps.tile([BLOCK_UNITS, RECORDS], F32, name="sums")
-            nc.tensor.matmul(
-                e_ps[:], lhsT=w2_wide[:, b].rearrange("p k j -> p (k j)"), rhs=u_tiles[b][:], start=True, stop=True
-            )
-            e_tiles.append(e_ps)
-        scale, shift_pair = normalisation(
-            nc, small, e_tiles,
-            columns[:, :, GAMMA_ROWS[1]], minus_gammas[:, :, 1], beta_pairs[:, :, 1, :], EPS / SELU_SCALE**2, minus_half,
-        )
-        y_tiles = activation(nc, work, e_tiles, scale, shift_pair)
 
         z_ps = once_ps.tile([RECORDS, NODES], F32, name="z_ps")
-        for b in range(BLOCKS):
-            z_block = z_ps[:, b * BLOCK_NODES : (b + 1) * BLOCK_NODES]
-            nc.tensor.matmul(z_block, lhsT=minus_alpha[:], rhs=w3_wide[:, b, :], start=True, stop=False)
-            nc.tensor.matmul(z_block, lhsT=y_tiles[b][:], rhs=w3_wide[:, b, :], start=False, stop=True)
+        items = [(layer, b) for layer in range(LAYERS) for b in range(BLOCKS)]
+        sources = list(a_tiles)
+        moments = [None] * BLOCKS
+        parts = [None] * BLOCKS
+        eps_of_layer = (EPS, EPS / SELU_SCALE**2)
+        for i in range(-STATISTICS_AHEAD, len(items) + 1):
+            if 0 <= i - 1 < len(items):
+                layer, b = items[i - 1]
+                both = selu_sum(nc, work, parts[b][0], parts[b][1])
+                if layer == 0:
+                    e_ps = layer_ps.tile([BLOCK_UNITS, RECORDS], F32, name="sums")
+                    nc.tensor.matmul(
+                        e_ps[:], lhsT=w2_wide[:, b].rearrange("p k j -> p (k j)"), rhs=both[:], start=True, stop=True
+                    )
+                    sources[b] = e_ps
+                else:
+                    z_block = z_ps[:, b * BLOCK_NODES : (b + 1) * BLOCK_NODES]
+                    nc.tensor.matmul(z_block, lhsT=minus_alpha[:], rhs=w3_wide[:, b, :], start=True, stop=False)
+                    nc.tensor.matmul(z_block, lhsT=both[:], rhs=w3_wide[:, b, :], start=False, stop=True)
+            if 0 <= i < len(items):
+                layer, b = items[i]
+                parts[b] = selu_parts(
+                    nc, small, work, sources[b], moments[b][0], moments[b][1],
+                    columns[:, b, GAMMA_ROWS[layer] : GAMMA_ROWS[layer] + 1], beta_pairs[:, b, layer, :],
+                )
+            if 0 <= i + STATISTICS_AHEAD < len(items):
+                layer, b = items[i + STATISTICS_AHEAD]
+                moments[b] = statistics(
+                    nc, small, sources[b], minus_gammas[:, b, layer : layer + 1], eps_of_layer[layer], minus_half
+                )
 
         result = held.tile([RECORDS, NODES], F32, name="result")
         nc.vector.scalar_tensor_tensor(

@@ -36,7 +36,7 @@ PARAM_SLOT = 32
 FLOPS = 2 * RECORDS * NODES * (PARENTS * HIDDEN + HIDDEN * HIDDEN + HIDDEN)
 
 
-def statistics(nc, small, source, minus_gamma, eps, minus_half):
+def normalise(nc, small, work, source, gamma, eps, minus_half):
     stats = small.tile([BLOCK_UNITS, 6], F32, name="stats")
     nc.vector.bn_stats(stats[:], source[:])
     mean_var = small.tile([BLOCK_UNITS, 2], F32, name="mean_var")
@@ -45,23 +45,16 @@ def statistics(nc, small, source, minus_gamma, eps, minus_half):
     nc.vector.tensor_scalar_add(var_eps[:], mean_var[:, 1:2], eps)
     rstd = small.tile([BLOCK_UNITS, 1], F32, name="rstd")
     nc.gpsimd.tensor_tensor(rstd[:], var_eps[:], minus_half[:], ALU.pow)
-    minus_mean_gamma = small.tile([BLOCK_UNITS, 1], F32, name="minus_mean_gamma")
-    nc.scalar.activation(minus_mean_gamma[:], mean_var[:, 0:1], FUNC.Identity, scale=minus_gamma)
-    return rstd, minus_mean_gamma
+    centred = work.tile([BLOCK_UNITS, RECORDS], F32, name="centred")
+    nc.vector.tensor_scalar(centred[:], source[:], mean_var[:, 0:1], gamma, op0=ALU.subtract, op1=ALU.mult)
+    return rstd, centred
 
 
-def selu_parts(nc, small, work, source, rstd, minus_mean_gamma, gamma, beta_pair):
-    scale = small.tile([BLOCK_UNITS, 1], F32, name="scale")
-    nc.scalar.activation(scale[:], rstd[:], FUNC.Identity, scale=gamma)
-    shift_pair = small.tile([BLOCK_UNITS, 2], F32, name="shift_pair")
-    for j in range(2):
-        nc.scalar.activation(
-            shift_pair[:, j : j + 1], rstd[:], FUNC.Identity, bias=beta_pair[:, j : j + 1], scale=minus_mean_gamma[:]
-        )
+def selu_parts(nc, work, rstd, centred, beta_pair):
     rise = work.tile([BLOCK_UNITS, RECORDS], F32, name="rise")
-    nc.scalar.activation(rise[:], source[:], FUNC.Relu, bias=shift_pair[:, 0:1], scale=scale[:])
+    nc.scalar.activation(rise[:], centred[:], FUNC.Relu, bias=beta_pair[:, 0:1], scale=rstd[:])
     grown = work.tile([BLOCK_UNITS, RECORDS], F32, name="grown")
-    nc.scalar.activation(grown[:], source[:], FUNC.Exp, bias=shift_pair[:, 1:2], scale=scale[:])
+    nc.scalar.activation(grown[:], centred[:], FUNC.Exp, bias=beta_pair[:, 1:2], scale=rstd[:])
     return rise, grown
 
 
@@ -138,8 +131,6 @@ def tile_customnetwork_kernel(tc, x, w1, gamma1, beta1, w2, gamma2, beta2, w3, b
         beta_pairs = held.tile([BLOCK_UNITS, BLOCKS, 2, 2], F32, name="beta_pairs")
         nc.scalar.copy(beta_pairs[:, :, :, 0], both_betas)
         nc.scalar.add(beta_pairs[:, :, :, 1], both_betas, math.log(SELU_ALPHA))
-        minus_gammas = held.tile([BLOCK_UNITS, BLOCKS, 2], F32, name="minus_gammas")
-        nc.scalar.mul(minus_gammas[:], columns[:, :, GAMMA_ROWS[0] : GAMMA_ROWS[1] + 1], -1.0)
         half_b3_last = held.tile([RECORDS, 1], F32, name="half_b3_last")
         nc.scalar.mul(half_b3_last[:], b3_copy[:, NODES - 1 : NODES], 0.5)
         same_node = columns[:, 0, NODE_ROWS : NODE_ROWS + BLOCK_NODES]
@@ -188,7 +179,7 @@ def tile_customnetwork_kernel(tc, x, w1, gamma1, beta1, w2, gamma2, beta2, w3, b
         z_ps = once_ps.tile([RECORDS, NODES], F32, name="z_ps")
         items = [(layer, b) for layer in range(LAYERS) for b in range(BLOCKS)]
         sources = list(a_tiles)
-        moments = [None] * BLOCKS
+        normalised = [None] * BLOCKS
         parts = [None] * BLOCKS
         eps_of_layer = (EPS, EPS / SELU_SCALE**2)
         for i in range(-STATISTICS_AHEAD, len(items) + 1):
@@ -207,14 +198,12 @@ def tile_customnetwork_kernel(tc, x, w1, gamma1, beta1, w2, gamma2, beta2, w3, b
                     nc.tensor.matmul(z_block, lhsT=both[:], rhs=w3_wide[:, b, :], start=False, stop=True)
             if 0 <= i < len(items):
                 layer, b = items[i]
-                parts[b] = selu_parts(
-                    nc, small, work, sources[b], moments[b][0], moments[b][1],
-                    columns[:, b, GAMMA_ROWS[layer] : GAMMA_ROWS[layer] + 1], beta_pairs[:, b, layer, :],
-                )
+                parts[b] = selu_parts(nc, work, normalised[b][0], normalised[b][1], beta_pairs[:, b, layer, :])
             if 0 <= i + STATISTICS_AHEAD < len(items):
                 layer, b = items[i + STATISTICS_AHEAD]
-                moments[b] = statistics(
-                    nc, small, sources[b], minus_gammas[:, b, layer : layer + 1], eps_of_layer[layer], minus_half
+                normalised[b] = normalise(
+                    nc, small, work, sources[b], columns[:, b, GAMMA_ROWS[layer] : GAMMA_ROWS[layer] + 1],
+                    eps_of_layer[layer], minus_half,
                 )
 
         result = held.tile([RECORDS, NODES], F32, name="result")

@@ -17,6 +17,7 @@ BLOCKS = 4
 BLOCK_NODES = NODES // BLOCKS
 BLOCK_UNITS = BLOCK_NODES * HIDDEN
 BLOCK_ENTRIES = BLOCK_NODES * PARENTS
+BLOCK_ORDER = (3, 0, 1, 2)
 LAYERS = 2
 STATISTICS_AHEAD = 2
 ENTRIES_PER_COLUMN = 16
@@ -79,14 +80,15 @@ def tile_customnetwork_kernel(tc, x, w1, gamma1, beta1, w2, gamma2, beta2, w3, b
         table = held.tile([RECORDS, GRAPH_NODES], F32, name="table")
         offsets = held.tile([RECORDS, NODES * PARENTS // ENTRIES_PER_COLUMN], U16, name="offsets")
         nc.scalar.dma_start(table[:], x)
+        first = BLOCK_ORDER[0]
         nc.sync.dma_start(
-            w1_copies[0][:, :half, :], w1_blocks[0][:, :half, :].to_broadcast([RECORDS, half, BLOCK_ENTRIES])
+            w1_copies[first][:, :half, :], w1_blocks[first][:, :half, :].to_broadcast([RECORDS, half, BLOCK_ENTRIES])
         )
         nc.sync.dma_start(offsets[:], offs)
         nc.sync.dma_start(
-            w1_copies[0][:, half:, :], w1_blocks[0][:, half:, :].to_broadcast([RECORDS, half, BLOCK_ENTRIES])
+            w1_copies[first][:, half:, :], w1_blocks[first][:, half:, :].to_broadcast([RECORDS, half, BLOCK_ENTRIES])
         )
-        for b in range(1, BLOCKS):
+        for b in BLOCK_ORDER[1:]:
             nc.sync.dma_start(w1_copies[b][:], w1_blocks[b].to_broadcast([RECORDS, HIDDEN, BLOCK_ENTRIES]))
         params = held.tile([PARAM_ROWS, NODES * HIDDEN], F32, name="params")
         nc.scalar.dma_start(params[W2_ROWS : W2_ROWS + HIDDEN, :], w2)
@@ -136,8 +138,8 @@ def tile_customnetwork_kernel(tc, x, w1, gamma1, beta1, w2, gamma2, beta2, w3, b
         same_node = columns[:, 0, NODE_ROWS : NODE_ROWS + BLOCK_NODES]
 
         columns_per_block = BLOCK_ENTRIES // ENTRIES_PER_COLUMN
-        a_tiles = []
-        for b in range(BLOCKS):
+        a_tiles = [None] * BLOCKS
+        for b in BLOCK_ORDER:
             piece = offsets[:, b * columns_per_block : (b + 1) * columns_per_block]
             products = work.tile([RECORDS, HIDDEN * BLOCK_ENTRIES], F32, name="products")
             for h in range(HIDDEN):
@@ -158,7 +160,7 @@ def tile_customnetwork_kernel(tc, x, w1, gamma1, beta1, w2, gamma2, beta2, w3, b
                     start=(d == 0),
                     stop=(d == PARENTS - 1),
                 )
-            a_tiles.append(a_ps)
+            a_tiles[b] = a_ps
 
         w2_wide = held.tile([BLOCK_UNITS, BLOCKS, HIDDEN, BLOCK_NODES], F32, name="w2_wide")
         w3_wide = held.tile([BLOCK_UNITS, BLOCKS, BLOCK_NODES], F32, name="w3_wide")
@@ -176,13 +178,31 @@ def tile_customnetwork_kernel(tc, x, w1, gamma1, beta1, w2, gamma2, beta2, w3, b
         )
 
 
-        z_ps = once_ps.tile([RECORDS, NODES], F32, name="z_ps")
-        items = [(layer, b) for layer in range(LAYERS) for b in range(BLOCKS)]
+        items = [(layer, b) for layer in range(LAYERS) for b in BLOCK_ORDER]
+        result = held.tile([RECORDS, NODES], F32, name="result")
+        z_tiles = [None] * BLOCKS
         sources = list(a_tiles)
         normalised = [None] * BLOCKS
         parts = [None] * BLOCKS
         eps_of_layer = (EPS, EPS / SELU_SCALE**2)
-        for i in range(-STATISTICS_AHEAD, len(items) + 1):
+        for i in range(-STATISTICS_AHEAD, len(items) + 2):
+            if LAYERS * BLOCKS - BLOCKS <= i - 2:
+                layer, b = items[i - 2]
+                plain = BLOCK_NODES - 1 if b == BLOCKS - 1 else BLOCK_NODES
+                nc.vector.scalar_tensor_tensor(
+                    out=result[:, b * BLOCK_NODES : b * BLOCK_NODES + plain],
+                    in0=z_tiles[b][:, :plain],
+                    scalar=SELU_SCALE,
+                    in1=b3_copy[:, b * BLOCK_NODES : b * BLOCK_NODES + plain],
+                    op0=ALU.mult,
+                    op1=ALU.add,
+                )
+                if b == BLOCKS - 1:
+                    tanh_half = held.tile([RECORDS, 1], F32, name="tanh_half")
+                    nc.scalar.activation(
+                        tanh_half[:], z_tiles[b][:, plain:], FUNC.Tanh, bias=half_b3_last[:], scale=0.5 * SELU_SCALE
+                    )
+                    nc.scalar.activation(result[:, NODES - 1 : NODES], tanh_half[:], FUNC.Identity, bias=0.5, scale=0.5)
             if 0 <= i - 1 < len(items):
                 layer, b = items[i - 1]
                 both = selu_sum(nc, work, parts[b][0], parts[b][1])
@@ -193,9 +213,9 @@ def tile_customnetwork_kernel(tc, x, w1, gamma1, beta1, w2, gamma2, beta2, w3, b
                     )
                     sources[b] = e_ps
                 else:
-                    z_block = z_ps[:, b * BLOCK_NODES : (b + 1) * BLOCK_NODES]
-                    nc.tensor.matmul(z_block, lhsT=minus_alpha[:], rhs=w3_wide[:, b, :], start=True, stop=False)
-                    nc.tensor.matmul(z_block, lhsT=both[:], rhs=w3_wide[:, b, :], start=False, stop=True)
+                    z_tiles[b] = layer_ps.tile([RECORDS, BLOCK_NODES], F32, name="sums")
+                    nc.tensor.matmul(z_tiles[b][:], lhsT=minus_alpha[:], rhs=w3_wide[:, b, :], start=True, stop=False)
+                    nc.tensor.matmul(z_tiles[b][:], lhsT=both[:], rhs=w3_wide[:, b, :], start=False, stop=True)
             if 0 <= i < len(items):
                 layer, b = items[i]
                 parts[b] = selu_parts(nc, work, normalised[b][0], normalised[b][1], beta_pairs[:, b, layer, :])
@@ -206,13 +226,4 @@ def tile_customnetwork_kernel(tc, x, w1, gamma1, beta1, w2, gamma2, beta2, w3, b
                     eps_of_layer[layer], minus_half,
                 )
 
-        result = held.tile([RECORDS, NODES], F32, name="result")
-        nc.vector.scalar_tensor_tensor(
-            out=result[:], in0=z_ps[:], scalar=SELU_SCALE, in1=b3_copy[:], op0=ALU.mult, op1=ALU.add
-        )
-        tanh_half = held.tile([RECORDS, 1], F32, name="tanh_half")
-        nc.scalar.activation(
-            tanh_half[:], z_ps[:, NODES - 1 : NODES], FUNC.Tanh, bias=half_b3_last[:], scale=0.5 * SELU_SCALE
-        )
-        nc.vector.tensor_scalar(result[:, NODES - 1 : NODES], tanh_half[:], 0.5, 0.5, op0=ALU.mult, op1=ALU.add)
         nc.sync.dma_start(out, result[:])

@@ -37,15 +37,12 @@ PARAM_SLOT = 32
 FLOPS = 2 * RECORDS * NODES * (PARENTS * HIDDEN + HIDDEN * HIDDEN + HIDDEN)
 
 
-def normalise(nc, small, work, source, gamma, eps, minus_half):
-    stats = small.tile([BLOCK_UNITS, 6], F32, name="stats")
-    nc.vector.bn_stats(stats[:], source[:])
+def normalise(nc, small, work, source, gamma, stats, minus_half):
+    nc.vector.bn_stats(stats[:, 0:6], source[:])
     mean_var = small.tile([BLOCK_UNITS, 2], F32, name="mean_var")
-    nc.vector.bn_aggr(mean_var[:], stats[:])
-    var_eps = small.tile([BLOCK_UNITS, 1], F32, name="var_eps")
-    nc.vector.tensor_scalar_add(var_eps[:], mean_var[:, 1:2], eps)
+    nc.vector.bn_aggr(mean_var[:], stats)
     rstd = small.tile([BLOCK_UNITS, 1], F32, name="rstd")
-    nc.gpsimd.tensor_tensor(rstd[:], var_eps[:], minus_half[:], ALU.pow)
+    nc.gpsimd.tensor_tensor(rstd[:], mean_var[:, 1:2], minus_half[:], ALU.pow)
     centred = work.tile([BLOCK_UNITS, RECORDS], F32, name="centred")
     nc.vector.tensor_scalar(centred[:], source[:], mean_var[:, 0:1], gamma, op0=ALU.subtract, op1=ALU.mult)
     return rstd, centred
@@ -103,6 +100,10 @@ def tile_customnetwork_kernel(tc, x, w1, gamma1, beta1, w2, gamma2, beta2, w3, b
         masks.make_identity(nc, identity[:])
         minus_half = held.tile([BLOCK_UNITS, 1], F32, name="minus_half")
         nc.vector.memset(minus_half[:], -0.5)
+        stats = held.tile([BLOCK_UNITS, LAYERS, BLOCKS, 9], F32, name="stats")
+        nc.vector.memset(stats[:, :, :, 6:8], 0.0)
+        for layer, eps in enumerate((EPS, EPS / SELU_SCALE**2)):
+            nc.vector.memset(stats[:, layer, :, 8:9], RECORDS * eps)
         minus_alpha = held.tile([BLOCK_UNITS, RECORDS], F32, name="minus_alpha")
         nc.vector.memset(minus_alpha[:], -SELU_ALPHA)
 
@@ -184,7 +185,6 @@ def tile_customnetwork_kernel(tc, x, w1, gamma1, beta1, w2, gamma2, beta2, w3, b
         sources = list(a_tiles)
         normalised = [None] * BLOCKS
         parts = [None] * BLOCKS
-        eps_of_layer = (EPS, EPS / SELU_SCALE**2)
         for i in range(-STATISTICS_AHEAD, len(items) + 2):
             if LAYERS * BLOCKS - BLOCKS <= i - 2:
                 layer, b = items[i - 2]
@@ -223,7 +223,7 @@ def tile_customnetwork_kernel(tc, x, w1, gamma1, beta1, w2, gamma2, beta2, w3, b
                 layer, b = items[i + STATISTICS_AHEAD]
                 normalised[b] = normalise(
                     nc, small, work, sources[b], columns[:, b, GAMMA_ROWS[layer] : GAMMA_ROWS[layer] + 1],
-                    eps_of_layer[layer], minus_half,
+                    stats[:, layer, b, :], minus_half,
                 )
 
         nc.sync.dma_start(out, result[:])

@@ -76,7 +76,7 @@ def tile_customnetwork_kernel(tc, x, w1, gamma1, beta1, w2, gamma2, beta2, w3, b
         w1_blocks = [w1[:, b * BLOCK_ENTRIES : (b + 1) * BLOCK_ENTRIES].unsqueeze(0) for b in range(BLOCKS)]
         table = held.tile([RECORDS, GRAPH_NODES], F32, name="table")
         offsets = held.tile([RECORDS, NODES * PARENTS // ENTRIES_PER_COLUMN], U16, name="offsets")
-        nc.scalar.dma_start(table[:], x)
+        nc.sync.dma_start(table[:], x)
         first = BLOCK_ORDER[0]
         nc.sync.dma_start(
             w1_copies[first][:, :half, :], w1_blocks[first][:, :half, :].to_broadcast([RECORDS, half, BLOCK_ENTRIES])

@@ -64,7 +64,6 @@ def selu_sum(nc, work, rise, grown):
 
 def tile_customnetwork_kernel(tc, x, w1, gamma1, beta1, w2, gamma2, beta2, w3, b3, offs, out):
     nc = tc.nc
-    half = HIDDEN // 2
     with (
         tc.tile_pool(name="held", bufs=1) as held,
         tc.tile_pool(name="work", bufs=2 * BLOCKS) as work,
@@ -78,13 +77,13 @@ def tile_customnetwork_kernel(tc, x, w1, gamma1, beta1, w2, gamma2, beta2, w3, b
         offsets = held.tile([RECORDS, NODES * PARENTS // ENTRIES_PER_COLUMN], U16, name="offsets")
         nc.sync.dma_start(table[:], x)
         first = BLOCK_ORDER[0]
-        nc.sync.dma_start(
-            w1_copies[first][:, :half, :], w1_blocks[first][:, :half, :].to_broadcast([RECORDS, half, BLOCK_ENTRIES])
-        )
-        nc.sync.dma_start(offsets[:], offs)
-        nc.sync.dma_start(
-            w1_copies[first][:, half:, :], w1_blocks[first][:, half:, :].to_broadcast([RECORDS, half, BLOCK_ENTRIES])
-        )
+        for run, (low, high) in enumerate(((0, 2), (2, 4), (4, HIDDEN))):
+            nc.sync.dma_start(
+                w1_copies[first][:, low:high, :],
+                w1_blocks[first][:, low:high, :].to_broadcast([RECORDS, high - low, BLOCK_ENTRIES]),
+            )
+            if run == 0:
+                nc.sync.dma_start(offsets[:], offs)
         for b in BLOCK_ORDER[1:]:
             nc.sync.dma_start(w1_copies[b][:], w1_blocks[b].to_broadcast([RECORDS, HIDDEN, BLOCK_ENTRIES]))
         params = held.tile([PARAM_ROWS, NODES * HIDDEN], F32, name="params")

@@ -48,11 +48,11 @@ def normalise(nc, small, work, source, gamma, stats, minus_half):
     return rstd, centred
 
 
-def selu_parts(nc, work, rstd, centred, beta_pair):
+def selu_parts(nc, work, rstd, centred, beta, beta_alpha):
     rise = work.tile([BLOCK_UNITS, RECORDS], F32, name="rise")
-    nc.scalar.activation(rise[:], centred[:], FUNC.Relu, bias=beta_pair[:, 0:1], scale=rstd[:])
+    nc.scalar.activation(rise[:], centred[:], FUNC.Relu, bias=beta, scale=rstd[:])
     grown = work.tile([BLOCK_UNITS, RECORDS], F32, name="grown")
-    nc.scalar.activation(grown[:], centred[:], FUNC.Exp, bias=beta_pair[:, 1:2], scale=rstd[:])
+    nc.scalar.activation(grown[:], centred[:], FUNC.Exp, bias=beta_alpha, scale=rstd[:])
     return rise, grown
 
 
@@ -88,10 +88,14 @@ def tile_customnetwork_kernel(tc, x, w1, gamma1, beta1, w2, gamma2, beta2, w3, b
             nc.sync.dma_start(w1_copies[b][:], w1_blocks[b].to_broadcast([RECORDS, HIDDEN, BLOCK_ENTRIES]))
         params = held.tile([PARAM_ROWS, NODES * HIDDEN], F32, name="params")
         nc.scalar.dma_start(params[W2_ROWS : W2_ROWS + HIDDEN, :], w2)
-        nc.scalar.dma_start(params[W3_ROW : W3_ROW + 1, :], w3)
-        for layer, (gamma, beta) in enumerate(((gamma1, beta1), (gamma2, beta2))):
-            nc.scalar.dma_start(params[GAMMA_ROWS[layer] : GAMMA_ROWS[layer] + 1, :], gamma)
-            nc.scalar.dma_start(params[BETA_ROWS[layer] : BETA_ROWS[layer] + 1, :], beta)
+        for queue, row, source in (
+            (nc.scalar, GAMMA_ROWS[0], gamma1),
+            (nc.scalar, BETA_ROWS[0], beta1),
+            (nc.sync, W3_ROW, w3),
+            (nc.sync, GAMMA_ROWS[1], gamma2),
+            (nc.sync, BETA_ROWS[1], beta2),
+        ):
+            queue.dma_start(params[row : row + 1, :], source)
         b3_copy = held.tile([RECORDS, NODES], F32, name="b3_copy")
         nc.sync.dma_start(b3_copy[:], b3.to_broadcast([RECORDS, NODES]))
 
@@ -130,9 +134,8 @@ def tile_customnetwork_kernel(tc, x, w1, gamma1, beta1, w2, gamma2, beta2, w3, b
         columns = held.tile([BLOCK_UNITS, BLOCKS, PARAM_SLOT], F32, name="columns")
         nc.scalar.copy(columns[:], columns_ps[:])
         both_betas = columns[:, :, BETA_ROWS[0] : BETA_ROWS[1] + 1]
-        beta_pairs = held.tile([BLOCK_UNITS, BLOCKS, 2, 2], F32, name="beta_pairs")
-        nc.scalar.copy(beta_pairs[:, :, :, 0], both_betas)
-        nc.scalar.add(beta_pairs[:, :, :, 1], both_betas, math.log(SELU_ALPHA))
+        beta_alphas = held.tile([BLOCK_UNITS, BLOCKS, LAYERS], F32, name="beta_alphas")
+        nc.scalar.add(beta_alphas[:], both_betas, math.log(SELU_ALPHA))
         half_b3_last = held.tile([RECORDS, 1], F32, name="half_b3_last")
         nc.scalar.mul(half_b3_last[:], b3_copy[:, NODES - 1 : NODES], 0.5)
         same_node = columns[:, 0, NODE_ROWS : NODE_ROWS + BLOCK_NODES]
@@ -217,7 +220,10 @@ def tile_customnetwork_kernel(tc, x, w1, gamma1, beta1, w2, gamma2, beta2, w3, b
                     nc.tensor.matmul(z_tiles[b][:], lhsT=both[:], rhs=w3_wide[:, b, :], start=False, stop=True)
             if 0 <= i < len(items):
                 layer, b = items[i]
-                parts[b] = selu_parts(nc, work, normalised[b][0], normalised[b][1], beta_pairs[:, b, layer, :])
+                parts[b] = selu_parts(
+                    nc, work, normalised[b][0], normalised[b][1],
+                    columns[:, b, BETA_ROWS[layer] : BETA_ROWS[layer] + 1], beta_alphas[:, b, layer : layer + 1],
+                )
             if 0 <= i + STATISTICS_AHEAD < len(items):
                 layer, b = items[i + STATISTICS_AHEAD]
                 normalised[b] = normalise(

@@ -77,7 +77,7 @@ def tile_customnetwork_kernel(tc, x, w1, gamma1, beta1, w2, gamma2, beta2, w3, b
         offsets = held.tile([RECORDS, NODES * PARENTS // ENTRIES_PER_COLUMN], U16, name="offsets")
         nc.sync.dma_start(table[:], x)
         first = BLOCK_ORDER[0]
-        for run, (low, high) in enumerate(((0, 2), (2, 4), (4, HIDDEN))):
+        for run, (low, high) in enumerate(((0, HIDDEN // 2), (HIDDEN // 2, HIDDEN))):
             nc.sync.dma_start(
                 w1_copies[first][:, low:high, :],
                 w1_blocks[first][:, low:high, :].to_broadcast([RECORDS, high - low, BLOCK_ENTRIES]),
@@ -117,22 +117,24 @@ def tile_customnetwork_kernel(tc, x, w1, gamma1, beta1, w2, gamma2, beta2, w3, b
             .unsqueeze(3)
             .to_broadcast([BLOCK_NODES, BLOCKS, BLOCK_NODES, HIDDEN]),
         )
-        params_by_unit = held.tile([PARAM_ROWS, NODES * HIDDEN], F32, name="params_by_unit")
+        params_by_unit = held.tile([128, NODES * HIDDEN], F32, name="params_by_unit")
+        nc.vector.memset(params_by_unit[:], 0.0)
         nc.scalar.copy(
-            params_by_unit[:].rearrange("p (b h i) -> p b h i", b=BLOCKS, h=HIDDEN),
+            params_by_unit[0:PARAM_ROWS, :].rearrange("p (b h i) -> p b h i", b=BLOCKS, h=HIDDEN),
             params[:].rearrange("p (b i h) -> p b h i", b=BLOCKS, h=HIDDEN),
         )
-        columns_ps = once_ps.tile([BLOCK_UNITS, BLOCKS, PARAM_SLOT], F32, name="columns_ps")
+        columns_ps = once_ps.tile([BLOCK_UNITS, BLOCKS, 128], F32, name="columns_ps")
         for b in range(BLOCKS):
             nc.tensor.matmul(
                 columns_ps[:, b, :],
                 lhsT=params_by_unit[:, b * BLOCK_UNITS : (b + 1) * BLOCK_UNITS],
-                rhs=identity[0:PARAM_ROWS, 0:PARAM_SLOT],
+                rhs=identity[:],
+                is_transpose=True,
                 start=True,
                 stop=True,
             )
         columns = held.tile([BLOCK_UNITS, BLOCKS, PARAM_SLOT], F32, name="columns")
-        nc.scalar.copy(columns[:], columns_ps[:])
+        nc.scalar.copy(columns[:], columns_ps[:, :, :PARAM_SLOT])
         both_betas = columns[:, :, BETA_ROWS[0] : BETA_ROWS[1] + 1]
         beta_alphas = held.tile([BLOCK_UNITS, BLOCKS, LAYERS], F32, name="beta_alphas")
         nc.scalar.add(beta_alphas[:], both_betas, math.log(SELU_ALPHA))

@@ -64,6 +64,7 @@ def selu_sum(nc, work, rise, grown):
 
 def tile_customnetwork_kernel(tc, x, w1, gamma1, beta1, w2, gamma2, beta2, w3, b3, offs, out):
     nc = tc.nc
+    half = HIDDEN // 2
     with (
         tc.tile_pool(name="held", bufs=1) as held,
         tc.tile_pool(name="work", bufs=2 * BLOCKS) as work,
@@ -77,25 +78,21 @@ def tile_customnetwork_kernel(tc, x, w1, gamma1, beta1, w2, gamma2, beta2, w3, b
         offsets = held.tile([RECORDS, NODES * PARENTS // ENTRIES_PER_COLUMN], U16, name="offsets")
         nc.sync.dma_start(table[:], x)
         first = BLOCK_ORDER[0]
-        for run, (low, high) in enumerate(((0, HIDDEN // 2), (HIDDEN // 2, HIDDEN))):
-            nc.sync.dma_start(
-                w1_copies[first][:, low:high, :],
-                w1_blocks[first][:, low:high, :].to_broadcast([RECORDS, high - low, BLOCK_ENTRIES]),
-            )
-            if run == 0:
-                nc.sync.dma_start(offsets[:], offs)
+        nc.sync.dma_start(
+            w1_copies[first][:, :half, :], w1_blocks[first][:, :half, :].to_broadcast([RECORDS, half, BLOCK_ENTRIES])
+        )
+        nc.sync.dma_start(offsets[:], offs)
+        nc.sync.dma_start(
+            w1_copies[first][:, half:, :], w1_blocks[first][:, half:, :].to_broadcast([RECORDS, half, BLOCK_ENTRIES])
+        )
         for b in BLOCK_ORDER[1:]:
             nc.sync.dma_start(w1_copies[b][:], w1_blocks[b].to_broadcast([RECORDS, HIDDEN, BLOCK_ENTRIES]))
         params = held.tile([PARAM_ROWS, NODES * HIDDEN], F32, name="params")
         nc.scalar.dma_start(params[W2_ROWS : W2_ROWS + HIDDEN, :], w2)
-        for queue, row, source in (
-            (nc.scalar, GAMMA_ROWS[0], gamma1),
-            (nc.scalar, BETA_ROWS[0], beta1),
-            (nc.sync, W3_ROW, w3),
-            (nc.sync, GAMMA_ROWS[1], gamma2),
-            (nc.sync, BETA_ROWS[1], beta2),
-        ):
-            queue.dma_start(params[row : row + 1, :], source)
+        nc.scalar.dma_start(params[W3_ROW : W3_ROW + 1, :], w3)
+        for layer, (gamma, beta) in enumerate(((gamma1, beta1), (gamma2, beta2))):
+            nc.scalar.dma_start(params[GAMMA_ROWS[layer] : GAMMA_ROWS[layer] + 1, :], gamma)
+            nc.scalar.dma_start(params[BETA_ROWS[layer] : BETA_ROWS[layer] + 1, :], beta)
         b3_copy = held.tile([RECORDS, NODES], F32, name="b3_copy")
         nc.sync.dma_start(b3_copy[:], b3.to_broadcast([RECORDS, NODES]))
 

import math

import concourse.masks as masks
import concourse.mybir as mybir

F32 = mybir.dt.float32
U16 = mybir.dt.uint16
ALU = mybir.AluOpType
FUNC = mybir.ActivationFunctionType

RECORDS = 128
GRAPH_NODES = 512
NODES = 64
PARENTS = 8
HIDDEN = 8
BLOCKS = 4
BLOCK_NODES = NODES // BLOCKS
BLOCK_UNITS = BLOCK_NODES * HIDDEN
BLOCK_ENTRIES = BLOCK_NODES * PARENTS
BLOCK_ORDER = (3, 0, 1, 2)
LAYERS = 2
STATISTICS_AHEAD = 2
ENTRIES_PER_COLUMN = 16

EPS = 1e-5
SELU_ALPHA = 1.6732632423543772
SELU_SCALE = 1.0507009873554805

NODE_ROWS = 0
W2_ROWS = 16
W3_ROW = 24
GAMMA_ROWS = (25, 26)
BETA_ROWS = (27, 28)
PARAM_ROWS = 29
PARAM_SLOT = 32

FLOPS = 2 * RECORDS * NODES * (PARENTS * HIDDEN + HIDDEN * HIDDEN + HIDDEN)


def normalise(nc, small, work, source, gamma, stats, minus_half):
    nc.vector.bn_stats(stats[:, 0:6], source[:])
    mean_var = small.tile([BLOCK_UNITS, 2], F32, name="mean_var")
    nc.vector.bn_aggr(mean_var[:], stats)
    rstd = small.tile([BLOCK_UNITS, 1], F32, name="rstd")
    nc.gpsimd.tensor_tensor(rstd[:], mean_var[:, 1:2], minus_half[:], ALU.pow)
    centred = work.tile([BLOCK_UNITS, RECORDS], F32, name="centred")
    nc.vector.tensor_scalar(centred[:], source[:], mean_var[:, 0:1], gamma, op0=ALU.subtract, op1=ALU.mult)
    return rstd, centred


def selu_parts(nc, work, rstd, centred, beta, beta_alpha):
    rise = work.tile([BLOCK_UNITS, RECORDS], F32, name="rise")
    nc.scalar.activation(rise[:], centred[:], FUNC.Relu, bias=beta, scale=rstd[:])
    grown = work.tile([BLOCK_UNITS, RECORDS], F32, name="grown")
    nc.scalar.activation(grown[:], centred[:], FUNC.Exp, bias=beta_alpha, scale=rstd[:])
    return rise, grown


def selu_sum(nc, work, rise, grown):
    both = work.tile([BLOCK_UNITS, RECORDS], F32, name="both")
    nc.vector.scalar_tensor_tensor(out=both[:], in0=grown[:], scalar=SELU_ALPHA, in1=rise[:], op0=ALU.min, op1=ALU.add)
    return both


def tile_customnetwork_kernel(tc, x, w1, gamma1, beta1, w2, gamma2, beta2, w3, b3, offs, out):
    nc = tc.nc
    half = HIDDEN // 2
    with (
        tc.tile_pool(name="held", bufs=1) as held,
        tc.tile_pool(name="work", bufs=2 * BLOCKS) as work,
        tc.tile_pool(name="small", bufs=2 * BLOCKS) as small,
        tc.psum_pool(name="once_ps", bufs=1) as once_ps,
        tc.psum_pool(name="layer_ps", bufs=6) as layer_ps,
    ):
        w1_copies = [held.tile([RECORDS, HIDDEN, BLOCK_ENTRIES], F32, name=f"w1_copy{b}") for b in range(BLOCKS)]
        w1_blocks = [w1[:, b * BLOCK_ENTRIES : (b + 1) * BLOCK_ENTRIES].unsqueeze(0) for b in range(BLOCKS)]
        table = held.tile([RECORDS, GRAPH_NODES], F32, name="table")
        offsets = held.tile([RECORDS, NODES * PARENTS // ENTRIES_PER_COLUMN], U16, name="offsets")
        nc.sync.dma_start(table[:], x)
        first = BLOCK_ORDER[0]
        nc.sync.dma_start(
            w1_copies[first][:, :half, :], w1_blocks[first][:, :half, :].to_broadcast([RECORDS, half, BLOCK_ENTRIES])
        )
        nc.sync.dma_start(offsets[:], offs)
        nc.sync.dma_start(
            w1_copies[first][:, half:, :], w1_blocks[first][:, half:, :].to_broadcast([RECORDS, half, BLOCK_ENTRIES])
        )
        for b in BLOCK_ORDER[1:]:
            nc.sync.dma_start(w1_copies[b][:], w1_blocks[b].to_broadcast([RECORDS, HIDDEN, BLOCK_ENTRIES]))
        params = held.tile([PARAM_ROWS, NODES * HIDDEN], F32, name="params")
        nc.scalar.dma_start(params[W2_ROWS : W2_ROWS + HIDDEN, :], w2)
        nc.scalar.dma_start(params[W3_ROW : W3_ROW + 1, :], w3)
        for layer, (gamma, beta) in enumerate(((gamma1, beta1), (gamma2, beta2))):
            nc.scalar.dma_start(params[GAMMA_ROWS[layer] : GAMMA_ROWS[layer] + 1, :], gamma)
            nc.scalar.dma_start(params[BETA_ROWS[layer] : BETA_ROWS[layer] + 1, :], beta)
        b3_copy = held.tile([RECORDS, NODES], F32, name="b3_copy")
        nc.sync.dma_start(b3_copy[:], b3.to_broadcast([RECORDS, NODES]))

        identity = held.tile([128, 128], F32, name="identity")
        masks.make_identity(nc, identity[:])
        minus_half = held.tile([BLOCK_UNITS, 1], F32, name="minus_half")
        nc.vector.memset(minus_half[:], -0.5)
        stats = held.tile([BLOCK_UNITS, LAYERS, BLOCKS, 9], F32, name="stats")
        nc.vector.memset(stats[:, :, :, 6:8], 0.0)
        for layer, eps in enumerate((EPS, EPS / SELU_SCALE**2)):
            nc.vector.memset(stats[:, layer, :, 8:9], RECORDS * eps)
        minus_alpha = held.tile([BLOCK_UNITS, RECORDS], F32, name="minus_alpha")
        nc.vector.memset(minus_alpha[:], -SELU_ALPHA)

        nc.scalar.copy(
            params[NODE_ROWS : NODE_ROWS + BLOCK_NODES, :].rearrange("p (b i h) -> p b i h", b=BLOCKS, h=HIDDEN),
            identity[0:BLOCK_NODES, 0:BLOCK_NODES]
            .unsqueeze(1)
            .unsqueeze(3)
            .to_broadcast([BLOCK_NODES, BLOCKS, BLOCK_NODES, HIDDEN]),
        )
        params_by_unit = held.tile([128, NODES * HIDDEN], F32, name="params_by_unit")
        nc.vector.memset(params_by_unit[:], 0.0)
        nc.scalar.copy(
            params_by_unit[0:PARAM_ROWS, :].rearrange("p (b h i) -> p b h i", b=BLOCKS, h=HIDDEN),
            params[:].rearrange("p (b i h) -> p b h i", b=BLOCKS, h=HIDDEN),
        )
        columns_ps = once_ps.tile([BLOCK_UNITS, BLOCKS, 128], F32, name="columns_ps")
        for b in range(BLOCKS):
            nc.tensor.matmul(
                columns_ps[:, b, :],
                lhsT=params_by_unit[:, b * BLOCK_UNITS : (b + 1) * BLOCK_UNITS],
                rhs=identity[:],
                is_transpose=True,
                start=True,
                stop=True,
            )
        columns = held.tile([BLOCK_UNITS, BLOCKS, PARAM_SLOT], F32, name="columns")
        nc.scalar.copy(columns[:], columns_ps[:, :, :PARAM_SLOT])
        both_betas = columns[:, :, BETA_ROWS[0] : BETA_ROWS[1] + 1]
        beta_alphas = held.tile([BLOCK_UNITS, BLOCKS, LAYERS], F32, name="beta_alphas")
        nc.scalar.add(beta_alphas[:], both_betas, math.log(SELU_ALPHA))
        half_b3_last = held.tile([RECORDS, 1], F32, name="half_b3_last")
        nc.scalar.mul(half_b3_last[:], b3_copy[:, NODES - 1 : NODES], 0.5)
        same_node = columns[:, 0, NODE_ROWS : NODE_ROWS + BLOCK_NODES]

        columns_per_block = BLOCK_ENTRIES // ENTRIES_PER_COLUMN
        a_tiles = [None] * BLOCKS
        for b in BLOCK_ORDER:
            piece = offsets[:, b * columns_per_block : (b + 1) * columns_per_block]
            products = work.tile([RECORDS, HIDDEN * BLOCK_ENTRIES], F32, name="products")
            for h in range(HIDDEN):
                nc.vector.tensor_tensor(
                    products[:, h * BLOCK_ENTRIES : (h + 1) * BLOCK_ENTRIES],
                    table[:].indirect(piece),
                    w1_copies[b][:, h, :],
                    ALU.mult,
                )
            by_parent = products[:].rearrange("r (u d) -> r u d", d=PARENTS)
            a_ps = layer_ps.tile([BLOCK_UNITS, RECORDS], F32, name="sums")
            for d in range(PARENTS):
                nc.tensor.matmul(
                    a_ps[:],
                    lhsT=by_parent[:, :, d],
                    rhs=identity[:],
                    is_transpose=True,
                    start=(d == 0),
                    stop=(d == PARENTS - 1),
                )
            a_tiles[b] = a_ps

        w2_wide = held.tile([BLOCK_UNITS, BLOCKS, HIDDEN, BLOCK_NODES], F32, name="w2_wide")
        w3_wide = held.tile([BLOCK_UNITS, BLOCKS, BLOCK_NODES], F32, name="w3_wide")
        nc.vector.tensor_tensor(
            w2_wide[:],
            same_node.unsqueeze(1).unsqueeze(1).to_broadcast([BLOCK_UNITS, BLOCKS, HIDDEN, BLOCK_NODES]),
            columns[:, :, W2_ROWS : W2_ROWS + HIDDEN].unsqueeze(3).to_broadcast([BLOCK_UNITS, BLOCKS, HIDDEN, BLOCK_NODES]),
            ALU.mult,
        )
        nc.vector.tensor_tensor(
            w3_wide[:],
            same_node.unsqueeze(1).to_broadcast([BLOCK_UNITS, BLOCKS, BLOCK_NODES]),
            columns[:, :, W3_ROW : W3_ROW + 1].to_broadcast([BLOCK_UNITS, BLOCKS, BLOCK_NODES]),
            ALU.mult,
        )


        items = [(layer, b) for layer in range(LAYERS) for b in BLOCK_ORDER]
        result = held.tile([RECORDS, NODES], F32, name="result")
        z_tiles = [None] * BLOCKS
        sources = list(a_tiles)
        normalised = [None] * BLOCKS
        parts = [None] * BLOCKS
        for i in range(-STATISTICS_AHEAD, len(items) + 2):
            if LAYERS * BLOCKS - BLOCKS <= i - 2:
                layer, b = items[i - 2]
                plain = BLOCK_NODES - 1 if b == BLOCKS - 1 else BLOCK_NODES
                nc.vector.scalar_tensor_tensor(
                    out=result[:, b * BLOCK_NODES : b * BLOCK_NODES + plain],
                    in0=z_tiles[b][:, :plain],
                    scalar=SELU_SCALE,
                    in1=b3_copy[:, b * BLOCK_NODES : b * BLOCK_NODES + plain],
                    op0=ALU.mult,
                    op1=ALU.add,
                )
                if b == BLOCKS - 1:
                    tanh_half = held.tile([RECORDS, 1], F32, name="tanh_half")
                    nc.scalar.activation(
                        tanh_half[:], z_tiles[b][:, plain:], FUNC.Tanh, bias=half_b3_last[:], scale=0.5 * SELU_SCALE
                    )
                    nc.scalar.activation(result[:, NODES - 1 : NODES], tanh_half[:], FUNC.Identity, bias=0.5, scale=0.5)
            if 0 <= i - 1 < len(items):
                layer, b = items[i - 1]
                both = selu_sum(nc, work, parts[b][0], parts[b][1])
                if layer == 0:
                    e_ps = layer_ps.tile([BLOCK_UNITS, RECORDS], F32, name="sums")
                    nc.tensor.matmul(
                        e_ps[:], lhsT=w2_wide[:, b].rearrange("p k j -> p (k j)"), rhs=both[:], start=True, stop=True
                    )
                    sources[b] = e_ps
                else:
                    z_tiles[b] = layer_ps.tile([RECORDS, BLOCK_NODES], F32, name="sums")
                    nc.tensor.matmul(z_tiles[b][:], lhsT=minus_alpha[:], rhs=w3_wide[:, b, :], start=True, stop=False)
                    nc.tensor.matmul(z_tiles[b][:], lhsT=both[:], rhs=w3_wide[:, b, :], start=False, stop=True)
            if 0 <= i < len(items):
                layer, b = items[i]
                parts[b] = selu_parts(
                    nc, work, normalised[b][0], normalised[b][1],
                    columns[:, b, BETA_ROWS[layer] : BETA_ROWS[layer] + 1], beta_alphas[:, b, layer : layer + 1],
                )
            if 0 <= i + STATISTICS_AHEAD < len(items):
                layer, b = items[i + STATISTICS_AHEAD]
                normalised[b] = normalise(
                    nc, small, work, sources[b], columns[:, b, GAMMA_ROWS[layer] : GAMMA_ROWS[layer] + 1],
                    stats[:, layer, b, :], minus_half,
                )

        nc.sync.dma_start(out, result[:])
